import numpy as np
import ml_dtypes


def mxq(x, axis, fmt="e4m3"):
    dtype, down = {"e4m3": (ml_dtypes.float8_e4m3fn, 7), "e5m2": (ml_dtypes.float8_e5m2, 14)}[fmt]
    v = np.moveaxis(np.asarray(x, np.float32).astype(ml_dtypes.bfloat16).astype(np.float64), axis, -1)
    blocks = v.reshape(v.shape[:-1] + (-1, 32))
    amax = np.abs(blocks).max(-1, keepdims=True)
    byte = np.maximum(np.where(amax > 0, np.frexp(amax)[1] - 1 + 127, 0) - down, 1)
    scale = np.exp2(byte - 127.0)
    codes = (blocks / scale).astype(np.float32).astype(dtype).astype(np.float64)
    return np.moveaxis((codes * scale).reshape(v.shape), -1, axis)


WIDE = False


def mx_kscale(k):
    if not WIDE:
        return np.ones(k)
    levels = np.array([10, -10, 5, -5, 0])
    a = np.random.permutation(np.resize(levels, k // 512 * 4)).reshape(k // 512, 4)
    idx = np.arange(k)
    return np.exp2(a[idx // 512, idx % 128 // 32])


BF16 = ml_dtypes.bfloat16


def bf(x):
    return np.asarray(x, np.float32).astype(BF16)


def f64(x):
    return np.asarray(x).astype(np.float64)


E2M1 = np.array([0.0, 0.5, 1.0, 1.5, 2.0, 3.0, 4.0, 6.0, -0.0, -0.5, -1.0, -1.5, -2.0, -3.0, -4.0, -6.0])


def pack_weight(w, fmt):
    k, n = w.shape
    w = f64(bf(w)).reshape(k // 32, 32, n)
    amax = np.abs(w).max(1)
    if fmt == "e4m3":
        byte = np.frexp(amax)[1] - 1 + 127 - 7
    else:
        mant, ex = np.frexp(amax / 6.0)
        byte = np.where(mant > 0.5, ex, ex - 1) + 127
    byte = np.clip(np.where(amax > 0, byte, 1), 1, 254)
    scaled = (w * np.exp2(127.0 - byte)[:, None, :]).reshape(k, n).astype(np.float32)
    by_word = np.ascontiguousarray(scaled.reshape(k // 512, 128, 4, n).transpose(0, 1, 3, 2))
    if fmt == "e4m3":
        words = by_word.astype(ml_dtypes.float8_e4m3fn).view(np.uint8)
    else:
        c = by_word.astype(ml_dtypes.float4_e2m1fn).view(np.uint8) & 0xF
        words = c[..., 0::2] | (c[..., 1::2] << 4)
    return np.ascontiguousarray(words), np.ascontiguousarray(byte.astype(np.uint8).reshape(k // 512, 16, n))


def unpack_weight(words, scales, fmt):
    g, p, n, _ = words.shape
    if fmt == "e4m3":
        vals = np.ascontiguousarray(words).view(ml_dtypes.float8_e4m3fn).astype(np.float64)
    else:
        nib = np.empty((g, p, n, 4), np.uint8)
        nib[..., 0::2] = words & 0xF
        nib[..., 1::2] = words >> 4
        vals = E2M1[nib]
    vals = vals * np.repeat(np.exp2(scales.astype(np.float64) - 127.0), 8, axis=1)[..., None]
    return vals.transpose(0, 1, 3, 2).reshape(g * 512, n)

def pack4(w):
    words, scales = pack_weight(w, "e2m1")
    return words.reshape(words.shape[0], 128, -1), scales


def unpack4(words, scales):
    return unpack_weight(words.reshape(words.shape[0], 128, -1, 2), scales, "e2m1")


N, C, F, G = 512, 3, 1024, 1024
F2 = F + F
F3 = F2 + F


def silu(v):
    return v / (1.0 + np.exp(-v))


def setup_inputs():
    s = mx_kscale(G)
    h = bf(silu(1.4 * np.random.standard_normal((N, 1, G))) * s)
    mu_W = bf(np.random.standard_normal((N, C, F)))
    mu_VW = bf(np.sqrt(C) * np.random.standard_normal((N, 1, F)))
    q = bf(np.random.standard_normal((N, 1, F)))
    mu = bf(np.random.standard_normal((N, C, F)))
    W2 = np.random.standard_normal((F3, G)) / np.sqrt(G) / s
    words, scales = pack4(np.ascontiguousarray(W2.T))
    b2 = bf(0.2 * np.random.standard_normal(F3))
    return {"h": h,
            "mu_W": mu_W,
            "mu_VW": mu_VW,
            "q": q,
            "mu": mu,
            "W2_words": words,
            "W2_scales": scales,
            "b2": b2}


def reference(h, mu_W, mu_VW, q, mu, W2_words, W2_scales, b2):
    x = (mxq(f64(h), 2, "e4m3") @ unpack4(W2_words, W2_scales)) + f64(b2)
    dq_intra = x[..., :F]
    dmu_intra = x[..., F:F2] * f64(mu_W)
    dqmu_intra = x[..., F2:] * f64(mu_VW)
    q_out = f64(q) + dq_intra + dqmu_intra
    mu_out = f64(mu) + dmu_intra
    return q_out, mu_out

@@ -1,0 +1,158 @@
+from contextlib import ExitStack
+
+import concourse.mybir as mybir
+from concourse.masks import make_identity
+
+F32 = mybir.dt.float32
+BF16 = mybir.dt.bfloat16
+I32 = mybir.dt.int32
+U32 = mybir.dt.uint32
+U8 = mybir.dt.uint8
+FP8X4 = mybir.dt.float8_e4m3fn_x4
+FP4X4 = mybir.dt.float4_e2m1fn_x4
+ADD = mybir.AluOpType.add
+MULT = mybir.AluOpType.mult
+
+P = 128
+ATOMS = 512
+ATOM_TILES = ATOMS // P
+K = 1024
+K_PASS = 4 * P
+PASSES = K // K_PASS
+F = 1024
+XYZ = 3
+BANK = 512
+BANKS_PER_BLOCK = F // BANK
+WORDS_PER_PASS = K_PASS // 2
+
+FLOPS = 2 * ATOMS * K * 3 * F
+
+
+def load_weight(nc, keep, W2_words, W2_scales):
+    w_planes = keep.tile([P, PASSES, 3 * F], U8, align_bytes=64)
+    nc.vector.memset(w_planes[:].bitcast(I32), 0)
+    scale_rows = W2_scales.rearrange("g r n -> r g n")
+    for low_q in range(2):
+        for i in range(4):
+            nc.sync.dma_start(
+                out=w_planes[32 * low_q + i : P : 64].bitcast(I32),
+                in_=scale_rows[4 * low_q + i : 16 : 8].bitcast(I32),
+            )
+    w_words = keep.tile([P, PASSES, 2 * 3 * F], U8, align_bytes=64)
+    nc.sync.dma_start(out=w_words[:].bitcast(I32), in_=W2_words.rearrange("g p b -> p g b").bitcast(I32))
+    return w_words, w_planes
+
+
+def quantise_h(nc, keep, psum, h_sb, ident):
+    h_codes = keep.tile([P, PASSES, ATOMS], U32, align_bytes=64)
+    h_scales = keep.tile([P, PASSES, ATOMS], U8, align_bytes=64)
+    h_words = h_sb[:].bitcast(F32)
+    for g in range(PASSES):
+        grouped = keep.tile([P, ATOMS, 4], BF16, align_bytes=64, tag="grouped%d" % g)
+        grouped_words = grouped[:].rearrange("p n t -> p (n t)").bitcast(F32).rearrange("p (n u) -> p n u", u=2)
+        for half in range(2):
+            turned = psum.tile([P, 2, 2 * P], F32, tag="turned")
+            for u in range(2):
+                for j in range(2):
+                    nc.tensor.transpose(
+                        turned[:, u, P * j : P * (j + 1)],
+                        h_words[:, 2 * half + j, WORDS_PER_PASS * g + u : WORDS_PER_PASS * (g + 1) : 2],
+                        ident[:],
+                    )
+            nc.scalar.copy(
+                out=grouped_words[:, 2 * P * half : 2 * P * (half + 1), :],
+                in_=turned[:].rearrange("p u n -> p n u"),
+            )
+        nc.vector.quantize_mx(
+            out=h_codes[:, g, :].bitcast(FP8X4),
+            scales=h_scales[:, g, :],
+            in_=grouped[:].rearrange("p n t -> p (n t)"),
+        )
+    return h_codes, h_scales
+
+
+def tile_painnmixing_pb_kernel(tc, h, mu_W, mu_VW, q, mu, W2_words, W2_scales, b2, out_0, out_1):
+    nc = tc.nc
+    with ExitStack() as ctx:
+        keep = ctx.enter_context(tc.tile_pool(name="keep", bufs=1))
+        inputs = ctx.enter_context(tc.tile_pool(name="inputs", bufs=ATOM_TILES))
+        work = ctx.enter_context(tc.tile_pool(name="work", bufs=2))
+        psum = ctx.enter_context(tc.psum_pool(name="psum", bufs=2))
+
+        ident = keep.tile([P, P], F32)
+        make_identity(nc, ident[:])
+
+        h_sb = keep.tile([P, ATOM_TILES, K], BF16)
+        nc.sync.dma_start(out=h_sb[:], in_=h.rearrange("(p a) o k -> p a (o k)", a=ATOM_TILES))
+        w_words, w_planes = load_weight(nc, keep, W2_words, W2_scales)
+        bias_rows = keep.tile([P, 3 * F], BF16)
+        nc.scalar.dma_start(out=bias_rows[:], in_=b2.partition_broadcast(P))
+
+        muW_rows = mu_W.rearrange("(p a) c f -> p a c f", a=ATOM_TILES)
+        mu_rows = mu.rearrange("(p a) c f -> p a c f", a=ATOM_TILES)
+        gate_rows = mu_VW.rearrange("(p a) o f -> p a (o f)", a=ATOM_TILES)
+        q_rows = q.rearrange("(p a) o f -> p a (o f)", a=ATOM_TILES)
+        q_out_rows = out_0.rearrange("(p a) o f -> p a (o f)", a=ATOM_TILES)
+        mu_out_rows = out_1.rearrange("(p a) c f -> p a c f", a=ATOM_TILES)
+        muW_tiles, mu_tiles, gate_tiles, q_tiles = [], [], [], []
+        for a in range(ATOM_TILES):
+            muW_a = inputs.tile([P, XYZ, F], BF16)
+            mu_a = inputs.tile([P, XYZ, F], BF16)
+            gate_a = inputs.tile([P, F], BF16)
+            q_a = inputs.tile([P, F], BF16)
+            nc.sync.dma_start(out=muW_a[:], in_=muW_rows[:, a])
+            nc.sync.dma_start(out=mu_a[:], in_=mu_rows[:, a])
+            nc.sync.dma_start(out=gate_a[:], in_=gate_rows[:, a])
+            nc.sync.dma_start(out=q_a[:], in_=q_rows[:, a])
+            muW_tiles.append(muW_a)
+            mu_tiles.append(mu_a)
+            gate_tiles.append(gate_a)
+            q_tiles.append(q_a)
+
+        h_codes, h_scales = quantise_h(nc, keep, psum, h_sb, ident)
+
+        def x_block(a, first_channel, tag):
+            atoms = slice(P * a, P * (a + 1))
+            acc = psum.tile([P, BANK], F32, tag=tag, name="acc")
+            for g in range(PASSES):
+                nc.tensor.matmul_mx(
+                    out=acc[:],
+                    lhsT=h_codes[:, g, atoms].bitcast(FP8X4),
+                    lhsT_scale=h_scales[:, g, atoms],
+                    rhs=w_words[:, g, 2 * first_channel : 2 * (first_channel + BANK)].bitcast(FP4X4),
+                    rhs_scale=w_planes[:, g, first_channel : first_channel + BANK],
+                    start=(g == 0),
+                    stop=(g == PASSES - 1),
+                )
+            return acc
+
+        for a in range(ATOM_TILES):
+            mu_new = work.tile([P, XYZ, F], F32)
+            q_new = work.tile([P, F], F32)
+            for c in range(BANKS_PER_BLOCK):
+                cols = slice(BANK * c, BANK * (c + 1))
+                acc_q = x_block(a, BANK * c, "acc_q")
+                acc_mu = x_block(a, F + BANK * c, "acc_mu")
+                acc_gate = x_block(a, 2 * F + BANK * c, "acc_gate")
+
+                x_mu = work.tile([P, BANK], F32)
+                nc.vector.tensor_tensor(out=x_mu[:], in0=acc_mu[:], in1=bias_rows[:, F + BANK * c : F + BANK * (c + 1)], op=ADD)
+                nc.vector.tensor_tensor(
+                    out=mu_new[:, :, cols],
+                    in0=x_mu[:].unsqueeze(1).to_broadcast([P, XYZ, BANK]),
+                    in1=muW_tiles[a][:, :, cols],
+                    op=MULT,
+                )
+                nc.vector.tensor_tensor(out=mu_new[:, :, cols], in0=mu_new[:, :, cols], in1=mu_tiles[a][:, :, cols], op=ADD)
+
+                x_gate = work.tile([P, BANK], F32)
+                nc.vector.tensor_tensor(
+                    out=x_gate[:], in0=acc_gate[:], in1=bias_rows[:, 2 * F + BANK * c : 2 * F + BANK * (c + 1)], op=ADD
+                )
+                nc.vector.tensor_tensor(out=x_gate[:], in0=x_gate[:], in1=gate_tiles[a][:, cols], op=MULT)
+                x_q = work.tile([P, BANK], F32)
+                nc.vector.tensor_tensor(out=x_q[:], in0=acc_q[:], in1=bias_rows[:, cols], op=ADD)
+                nc.vector.tensor_tensor(out=x_q[:], in0=x_q[:], in1=q_tiles[a][:, cols], op=ADD)
+                nc.vector.tensor_tensor(out=q_new[:, cols], in0=x_q[:], in1=x_gate[:], op=ADD)
+            nc.sync.dma_start(out=mu_out_rows[:, a], in_=mu_new[:])
+            nc.sync.dma_start(out=q_out_rows[:, a], in_=q_new[:])

@@ -12,6 +12,7 @@ FP8X4 = mybir.dt.float8_e4m3fn_x4
 FP4X4 = mybir.dt.float4_e2m1fn_x4
 ADD = mybir.AluOpType.add
 MULT = mybir.AluOpType.mult
+IDENTITY = mybir.ActivationFunctionType.Identity
 
 P = 128
 ATOMS = 512
@@ -19,56 +20,18 @@ ATOM_TILES = ATOMS // P
 K = 1024
 K_PASS = 4 * P
 PASSES = K // K_PASS
+WORDS_PER_PASS = K_PASS // 2
 F = 1024
+Q_BLOCK = 0
+MU_BLOCK = 1
+GATE_BLOCK = 2
 XYZ = 3
 BANK = 512
-BANKS_PER_BLOCK = F // BANK
-WORDS_PER_PASS = K_PASS // 2
+HALVES = F // BANK
+CHANNEL_TILES = 3 * F // P
+TILES_PER_BANK = BANK // P
 
 FLOPS = 2 * ATOMS * K * 3 * F
-
-
-def load_weight(nc, keep, W2_words, W2_scales):
-    w_planes = keep.tile([P, PASSES, 3 * F], U8, align_bytes=64)
-    nc.vector.memset(w_planes[:].bitcast(I32), 0)
-    scale_rows = W2_scales.rearrange("g r n -> r g n")
-    for low_q in range(2):
-        for i in range(4):
-            nc.sync.dma_start(
-                out=w_planes[32 * low_q + i : P : 64].bitcast(I32),
-                in_=scale_rows[4 * low_q + i : 16 : 8].bitcast(I32),
-            )
-    w_words = keep.tile([P, PASSES, 2 * 3 * F], U8, align_bytes=64)
-    nc.sync.dma_start(out=w_words[:].bitcast(I32), in_=W2_words.rearrange("g p b -> p g b").bitcast(I32))
-    return w_words, w_planes
-
-
-def quantise_h(nc, keep, psum, h_sb, ident):
-    h_codes = keep.tile([P, PASSES, ATOMS], U32, align_bytes=64)
-    h_scales = keep.tile([P, PASSES, ATOMS], U8, align_bytes=64)
-    h_words = h_sb[:].bitcast(F32)
-    for g in range(PASSES):
-        grouped = keep.tile([P, ATOMS, 4], BF16, align_bytes=64, tag="grouped%d" % g)
-        grouped_words = grouped[:].rearrange("p n t -> p (n t)").bitcast(F32).rearrange("p (n u) -> p n u", u=2)
-        for half in range(2):
-            turned = psum.tile([P, 2, 2 * P], F32, tag="turned")
-            for u in range(2):
-                for j in range(2):
-                    nc.tensor.transpose(
-                        turned[:, u, P * j : P * (j + 1)],
-                        h_words[:, 2 * half + j, WORDS_PER_PASS * g + u : WORDS_PER_PASS * (g + 1) : 2],
-                        ident[:],
-                    )
-            nc.scalar.copy(
-                out=grouped_words[:, 2 * P * half : 2 * P * (half + 1), :],
-                in_=turned[:].rearrange("p u n -> p n u"),
-            )
-        nc.vector.quantize_mx(
-            out=h_codes[:, g, :].bitcast(FP8X4),
-            scales=h_scales[:, g, :],
-            in_=grouped[:].rearrange("p n t -> p (n t)"),
-        )
-    return h_codes, h_scales
 
 
 def tile_painnmixing_pb_kernel(tc, h, mu_W, mu_VW, q, mu, W2_words, W2_scales, b2, out_0, out_1):
@@ -76,83 +39,145 @@ def tile_painnmixing_pb_kernel(tc, h, mu_W, mu_VW, q, mu, W2_words, W2_scales, b
     with ExitStack() as ctx:
         keep = ctx.enter_context(tc.tile_pool(name="keep", bufs=1))
         inputs = ctx.enter_context(tc.tile_pool(name="inputs", bufs=ATOM_TILES))
-        work = ctx.enter_context(tc.tile_pool(name="work", bufs=2))
-        psum = ctx.enter_context(tc.psum_pool(name="psum", bufs=2))
+        mu_results = ctx.enter_context(tc.tile_pool(name="mu_results", bufs=ATOM_TILES))
+        q_results = ctx.enter_context(tc.tile_pool(name="q_results", bufs=2))
+        psum_acc = ctx.enter_context(tc.psum_pool(name="psum_acc", bufs=3))
+        psum_rows = ctx.enter_context(tc.psum_pool(name="psum_rows", bufs=5))
 
         ident = keep.tile([P, P], F32)
         make_identity(nc, ident[:])
 
         h_sb = keep.tile([P, ATOM_TILES, K], BF16)
-        nc.sync.dma_start(out=h_sb[:], in_=h.rearrange("(p a) o k -> p a (o k)", a=ATOM_TILES))
-        w_words, w_planes = load_weight(nc, keep, W2_words, W2_scales)
-        bias_rows = keep.tile([P, 3 * F], BF16)
-        nc.scalar.dma_start(out=bias_rows[:], in_=b2.partition_broadcast(P))
+        h_rows = h.rearrange("(p a) o k -> p a (o k)", a=ATOM_TILES)
+        for half in range(2):
+            nc.sync.dma_start(out=h_sb[:, 2 * half : 2 * half + 2, :], in_=h_rows[:, 2 * half : 2 * half + 2, :])
+
+        w_planes = keep.tile([P, PASSES, 3 * F], U8, align_bytes=64)
+        nc.vector.memset(w_planes[:].bitcast(I32), 0)
+        scale_rows = W2_scales.rearrange("g r n -> r g n")
+        for low_q in range(2):
+            for i in range(4):
+                nc.sync.dma_start(
+                    out=w_planes[32 * low_q + i : P : 64].bitcast(I32),
+                    in_=scale_rows[4 * low_q + i : 16 : 8].bitcast(I32),
+                )
+
+        word_rows = W2_words.rearrange("g p b -> p g b")
+
+        def load_words(block):
+            words = keep.tile([P, PASSES, 2 * F], U8, align_bytes=64, tag="words%d" % block)
+            nc.sync.dma_start(out=words[:].bitcast(I32), in_=word_rows[:, :, 2 * F * block : 2 * F * (block + 1)].bitcast(I32))
+            return words
 
         muW_rows = mu_W.rearrange("(p a) c f -> p a c f", a=ATOM_TILES)
         mu_rows = mu.rearrange("(p a) c f -> p a c f", a=ATOM_TILES)
-        gate_rows = mu_VW.rearrange("(p a) o f -> p a (o f)", a=ATOM_TILES)
-        q_rows = q.rearrange("(p a) o f -> p a (o f)", a=ATOM_TILES)
-        q_out_rows = out_0.rearrange("(p a) o f -> p a (o f)", a=ATOM_TILES)
-        mu_out_rows = out_1.rearrange("(p a) c f -> p a c f", a=ATOM_TILES)
-        muW_tiles, mu_tiles, gate_tiles, q_tiles = [], [], [], []
+        w_words = {MU_BLOCK: load_words(MU_BLOCK)}
+        muW_tiles, mu_tiles = [], []
         for a in range(ATOM_TILES):
             muW_a = inputs.tile([P, XYZ, F], BF16)
             mu_a = inputs.tile([P, XYZ, F], BF16)
-            gate_a = inputs.tile([P, F], BF16)
-            q_a = inputs.tile([P, F], BF16)
             nc.sync.dma_start(out=muW_a[:], in_=muW_rows[:, a])
             nc.sync.dma_start(out=mu_a[:], in_=mu_rows[:, a])
-            nc.sync.dma_start(out=gate_a[:], in_=gate_rows[:, a])
-            nc.sync.dma_start(out=q_a[:], in_=q_rows[:, a])
             muW_tiles.append(muW_a)
             mu_tiles.append(mu_a)
-            gate_tiles.append(gate_a)
-            q_tiles.append(q_a)
+            if a == 0:
+                w_words[GATE_BLOCK] = load_words(GATE_BLOCK)
+                w_words[Q_BLOCK] = load_words(Q_BLOCK)
+        gate_sb = keep.tile([P, ATOM_TILES, F], BF16)
+        q_sb = keep.tile([P, ATOM_TILES, F], BF16)
+        nc.sync.dma_start(out=gate_sb[:], in_=mu_VW.rearrange("(p a) o f -> p a (o f)", a=ATOM_TILES))
+        nc.sync.dma_start(out=q_sb[:], in_=q.rearrange("(p a) o f -> p a (o f)", a=ATOM_TILES))
 
-        h_codes, h_scales = quantise_h(nc, keep, psum, h_sb, ident)
+        bias_bf = keep.tile([P, P], BF16)
+        nc.vector.memset(bias_bf[:], 0.0)
+        nc.scalar.dma_start(out=bias_bf[:CHANNEL_TILES, :], in_=b2.rearrange("(j c) -> j c", c=P))
+        bias_f32 = keep.tile([P, P], F32)
+        nc.vector.tensor_copy(out=bias_f32[:], in_=bias_bf[:])
+        bias_turned = psum_acc.tile([P, P], F32, tag="acc")
+        nc.tensor.transpose(bias_turned[:], bias_f32[:], ident[:])
+        bias_col = keep.tile([P, CHANNEL_TILES], F32)
+        nc.scalar.activation(out=bias_col[:], in_=bias_turned[:, :CHANNEL_TILES], func=IDENTITY)
 
-        def x_block(a, first_channel, tag):
-            atoms = slice(P * a, P * (a + 1))
-            acc = psum.tile([P, BANK], F32, tag=tag, name="acc")
+        h_codes = keep.tile([P, PASSES, ATOMS], U32, align_bytes=64)
+        h_scales = keep.tile([P, PASSES, ATOMS], U8, align_bytes=64)
+        h_words = h_sb[:].bitcast(F32)
+        for half in range(2):
+            atoms = slice(2 * P * half, 2 * P * (half + 1))
             for g in range(PASSES):
-                nc.tensor.matmul_mx(
-                    out=acc[:],
-                    lhsT=h_codes[:, g, atoms].bitcast(FP8X4),
-                    lhsT_scale=h_scales[:, g, atoms],
-                    rhs=w_words[:, g, 2 * first_channel : 2 * (first_channel + BANK)].bitcast(FP4X4),
-                    rhs_scale=w_planes[:, g, first_channel : first_channel + BANK],
-                    start=(g == 0),
-                    stop=(g == PASSES - 1),
+                turned = psum_rows.tile([P, 2, 2 * P], F32, tag="x_rows")
+                for u in range(2):
+                    for j in range(2):
+                        nc.tensor.transpose(
+                            turned[:, u, P * j : P * (j + 1)],
+                            h_words[:, 2 * half + j, WORDS_PER_PASS * g + u : WORDS_PER_PASS * (g + 1) : 2],
+                            ident[:],
+                        )
+                grouped = keep.tile([P, 2 * P, 4], BF16, align_bytes=64, tag="grouped%d%d" % (half, g))
+                grouped_words = grouped[:].rearrange("p n t -> p (n t)").bitcast(F32).rearrange("p (n u) -> p n u", u=2)
+                if g == 0:
+                    nc.scalar.copy(out=grouped_words, in_=turned[:].rearrange("p u n -> p n u"))
+                else:
+                    nc.vector.tensor_copy(out=grouped_words, in_=turned[:].rearrange("p u n -> p n u"))
+                nc.vector.quantize_mx(
+                    out=h_codes[:, g, atoms].bitcast(FP8X4),
+                    scales=h_scales[:, g, atoms],
+                    in_=grouped[:].rearrange("p n t -> p (n t)"),
                 )
-            return acc
 
+        def make_x_columns(block, half):
+            x_cols = keep.tile([P, TILES_PER_BANK, ATOMS], F32, tag="x_cols%d%d" % (block, half))
+            for i in range(TILES_PER_BANK):
+                in_block = TILES_PER_BANK * half + i
+                j = F // P * block + in_block
+                acc = psum_acc.tile([P, ATOMS], F32, tag="acc")
+                for g in range(PASSES):
+                    nc.tensor.matmul_mx(
+                        out=acc[:],
+                        lhsT=w_words[block][:, g, 2 * P * in_block : 2 * P * (in_block + 1)].bitcast(FP4X4),
+                        lhsT_scale=w_planes[:, g, P * j : P * (j + 1)],
+                        rhs=h_codes[:, g, :].bitcast(FP8X4),
+                        rhs_scale=h_scales[:, g, :],
+                        start=(g == 0),
+                        stop=(g == PASSES - 1),
+                    )
+                nc.scalar.activation(out=x_cols[:, i, :], in_=acc[:], func=IDENTITY, bias=bias_col[:, j : j + 1])
+            return x_cols
+
+        def turn_back(x_cols, a):
+            x_rows = psum_rows.tile([P, BANK], F32, tag="x_rows")
+            for i in range(TILES_PER_BANK):
+                nc.tensor.transpose(x_rows[:, P * i : P * (i + 1)], x_cols[:, i, P * a : P * (a + 1)], ident[:])
+            return x_rows
+
+        x_cols_of = {}
+        for half in range(HALVES):
+            x_cols_of[MU_BLOCK, half] = make_x_columns(MU_BLOCK, half)
+        mu_out_rows = out_1.rearrange("(p a) c f -> p a c f", a=ATOM_TILES)
         for a in range(ATOM_TILES):
-            mu_new = work.tile([P, XYZ, F], F32)
-            q_new = work.tile([P, F], F32)
-            for c in range(BANKS_PER_BLOCK):
-                cols = slice(BANK * c, BANK * (c + 1))
-                acc_q = x_block(a, BANK * c, "acc_q")
-                acc_mu = x_block(a, F + BANK * c, "acc_mu")
-                acc_gate = x_block(a, 2 * F + BANK * c, "acc_gate")
-
-                x_mu = work.tile([P, BANK], F32)
-                nc.vector.tensor_tensor(out=x_mu[:], in0=acc_mu[:], in1=bias_rows[:, F + BANK * c : F + BANK * (c + 1)], op=ADD)
+            mu_new = mu_results.tile([P, XYZ, F], F32)
+            for half in range(HALVES):
+                cols = slice(BANK * half, BANK * (half + 1))
+                x_mu = turn_back(x_cols_of[MU_BLOCK, half], a)
                 nc.vector.tensor_tensor(
                     out=mu_new[:, :, cols],
                     in0=x_mu[:].unsqueeze(1).to_broadcast([P, XYZ, BANK]),
                     in1=muW_tiles[a][:, :, cols],
                     op=MULT,
                 )
-                nc.vector.tensor_tensor(out=mu_new[:, :, cols], in0=mu_new[:, :, cols], in1=mu_tiles[a][:, :, cols], op=ADD)
-
-                x_gate = work.tile([P, BANK], F32)
-                nc.vector.tensor_tensor(
-                    out=x_gate[:], in0=acc_gate[:], in1=bias_rows[:, 2 * F + BANK * c : 2 * F + BANK * (c + 1)], op=ADD
-                )
-                nc.vector.tensor_tensor(out=x_gate[:], in0=x_gate[:], in1=gate_tiles[a][:, cols], op=MULT)
-                x_q = work.tile([P, BANK], F32)
-                nc.vector.tensor_tensor(out=x_q[:], in0=acc_q[:], in1=bias_rows[:, cols], op=ADD)
-                nc.vector.tensor_tensor(out=x_q[:], in0=x_q[:], in1=q_tiles[a][:, cols], op=ADD)
-                nc.vector.tensor_tensor(out=q_new[:, cols], in0=x_q[:], in1=x_gate[:], op=ADD)
+                nc.gpsimd.tensor_tensor(out=mu_new[:, :, cols], in0=mu_new[:, :, cols], in1=mu_tiles[a][:, :, cols], op=ADD)
             nc.sync.dma_start(out=mu_out_rows[:, a], in_=mu_new[:])
+            block = (GATE_BLOCK, Q_BLOCK)[a % 2]
+            x_cols_of[block, a // 2] = make_x_columns(block, a // 2)
+
+        q_out_rows = out_0.rearrange("(p a) o f -> p a (o f)", a=ATOM_TILES)
+        for a in range(ATOM_TILES):
+            q_new = q_results.tile([P, F], F32)
+            q_plus_x = q_results.tile([P, F], F32)
+            for half in range(HALVES):
+                cols = slice(BANK * half, BANK * (half + 1))
+                x_q = turn_back(x_cols_of[Q_BLOCK, half], a)
+                nc.vector.tensor_tensor(out=q_plus_x[:, cols], in0=x_q[:], in1=q_sb[:, a, cols], op=ADD)
+                x_gate = turn_back(x_cols_of[GATE_BLOCK, half], a)
+                nc.vector.tensor_tensor(out=q_new[:, cols], in0=x_gate[:], in1=gate_sb[:, a, cols], op=MULT)
+            nc.vector.tensor_tensor(out=q_new[:], in0=q_new[:], in1=q_plus_x[:], op=ADD)
             nc.sync.dma_start(out=q_out_rows[:, a], in_=q_new[:])

@@ -43,6 +43,7 @@ def tile_painnmixing_pb_kernel(tc, h, mu_W, mu_VW, q, mu, W2_words, W2_scales, b
         q_results = ctx.enter_context(tc.tile_pool(name="q_results", bufs=2))
         psum_acc = ctx.enter_context(tc.psum_pool(name="psum_acc", bufs=3))
         psum_rows = ctx.enter_context(tc.psum_pool(name="psum_rows", bufs=5))
+        ctx.enter_context(tc.manual_schedule())
 
         ident = keep.tile([P, P], F32)
         make_identity(nc, ident[:])
@@ -164,8 +165,10 @@ def tile_painnmixing_pb_kernel(tc, h, mu_W, mu_VW, q, mu, W2_words, W2_scales, b
                     in1=muW_tiles[a][:, :, cols],
                     op=MULT,
                 )
-                nc.gpsimd.tensor_tensor(out=mu_new[:, :, cols], in0=mu_new[:, :, cols], in1=mu_tiles[a][:, :, cols], op=ADD)
-            nc.sync.dma_start(out=mu_out_rows[:, a], in_=mu_new[:])
+                last_but_one = a == ATOM_TILES - 1 and half == HALVES - 2
+                adder = nc.vector if last_but_one else nc.gpsimd
+                adder.tensor_tensor(out=mu_new[:, :, cols], in0=mu_new[:, :, cols], in1=mu_tiles[a][:, :, cols], op=ADD)
+                nc.sync.dma_start(out=mu_out_rows[:, a, :, cols], in_=mu_new[:, :, cols])
             block = (GATE_BLOCK, Q_BLOCK)[a % 2]
             x_cols_of[block, a // 2] = make_x_columns(block, a // 2)
 
@@ -180,4 +183,4 @@ def tile_painnmixing_pb_kernel(tc, h, mu_W, mu_VW, q, mu, W2_words, W2_scales, b
                 x_gate = turn_back(x_cols_of[GATE_BLOCK, half], a)
                 nc.vector.tensor_tensor(out=q_new[:, cols], in0=x_gate[:], in1=gate_sb[:, a, cols], op=MULT)
             nc.vector.tensor_tensor(out=q_new[:], in0=q_new[:], in1=q_plus_x[:], op=ADD)
-            nc.sync.dma_start(out=q_out_rows[:, a], in_=q_new[:])
+            nc.scalar.dma_start(out=q_out_rows[:, a], in_=q_new[:])

@@ -47,6 +47,8 @@ def tile_painnmixing_pb_kernel(tc, h, mu_W, mu_VW, q, mu, W2_words, W2_scales, b
 
         ident = keep.tile([P, P], F32)
         make_identity(nc, ident[:])
+        ident_bf = keep.tile([P, P], BF16)
+        make_identity(nc, ident_bf[:])
 
         h_sb = keep.tile([P, ATOM_TILES, K], BF16)
         h_rows = h.rearrange("(p a) o k -> p a (o k)", a=ATOM_TILES)
@@ -165,9 +167,7 @@ def tile_painnmixing_pb_kernel(tc, h, mu_W, mu_VW, q, mu, W2_words, W2_scales, b
                     in1=muW_tiles[a][:, :, cols],
                     op=MULT,
                 )
-                last_but_one = a == ATOM_TILES - 1 and half == HALVES - 2
-                adder = nc.vector if last_but_one else nc.gpsimd
-                adder.tensor_tensor(out=mu_new[:, :, cols], in0=mu_new[:, :, cols], in1=mu_tiles[a][:, :, cols], op=ADD)
+                nc.gpsimd.tensor_tensor(out=mu_new[:, :, cols], in0=mu_new[:, :, cols], in1=mu_tiles[a][:, :, cols], op=ADD)
                 nc.sync.dma_start(out=mu_out_rows[:, a, :, cols], in_=mu_new[:, :, cols])
             block = (GATE_BLOCK, Q_BLOCK)[a % 2]
             x_cols_of[block, a // 2] = make_x_columns(block, a // 2)
@@ -175,12 +175,22 @@ def tile_painnmixing_pb_kernel(tc, h, mu_W, mu_VW, q, mu, W2_words, W2_scales, b
         q_out_rows = out_0.rearrange("(p a) o f -> p a (o f)", a=ATOM_TILES)
         for a in range(ATOM_TILES):
             q_new = q_results.tile([P, F], F32)
-            q_plus_x = q_results.tile([P, F], F32)
             for half in range(HALVES):
                 cols = slice(BANK * half, BANK * (half + 1))
-                x_q = turn_back(x_cols_of[Q_BLOCK, half], a)
-                nc.vector.tensor_tensor(out=q_plus_x[:, cols], in0=x_q[:], in1=q_sb[:, a, cols], op=ADD)
                 x_gate = turn_back(x_cols_of[GATE_BLOCK, half], a)
                 nc.vector.tensor_tensor(out=q_new[:, cols], in0=x_gate[:], in1=gate_sb[:, a, cols], op=MULT)
-            nc.vector.tensor_tensor(out=q_new[:], in0=q_new[:], in1=q_plus_x[:], op=ADD)
+            for half in range(HALVES):
+                cols = slice(BANK * half, BANK * (half + 1))
+                q_plus_x = psum_rows.tile([P, BANK], F32, tag="x_rows")
+                nc.tensor.matmul(out=q_plus_x[:], lhsT=ident_bf[:], rhs=q_sb[:, a, cols], start=True, stop=False)
+                for i in range(TILES_PER_BANK):
+                    nc.tensor.matmul(
+                        out=q_plus_x[:, P * i : P * (i + 1)],
+                        lhsT=x_cols_of[Q_BLOCK, half][:, i, P * a : P * (a + 1)],
+                        rhs=ident[:],
+                        is_transpose=True,
+                        start=False,
+                        stop=(i == TILES_PER_BANK - 1),
+                    )
+                nc.vector.tensor_tensor(out=q_new[:, cols], in0=q_plus_x[:], in1=q_new[:, cols], op=ADD)
             nc.scalar.dma_start(out=q_out_rows[:, a], in_=q_new[:])

@@ -27,6 +27,7 @@ MU_BLOCK = 1
 GATE_BLOCK = 2
 XYZ = 3
 BANK = 512
+PSUM_BANKS = 8
 HALVES = F // BANK
 CHANNEL_TILES = 3 * F // P
 TILES_PER_BANK = BANK // P
@@ -41,8 +42,7 @@ def tile_painnmixing_pb_kernel(tc, h, mu_W, mu_VW, q, mu, W2_words, W2_scales, b
         inputs = ctx.enter_context(tc.tile_pool(name="inputs", bufs=ATOM_TILES))
         mu_results = ctx.enter_context(tc.tile_pool(name="mu_results", bufs=ATOM_TILES))
         q_results = ctx.enter_context(tc.tile_pool(name="q_results", bufs=2))
-        psum_acc = ctx.enter_context(tc.psum_pool(name="psum_acc", bufs=3))
-        psum_rows = ctx.enter_context(tc.psum_pool(name="psum_rows", bufs=5))
+        psum = ctx.enter_context(tc.psum_pool(name="psum", bufs=PSUM_BANKS))
         ctx.enter_context(tc.manual_schedule())
 
         ident = keep.tile([P, P], F32)
@@ -52,8 +52,8 @@ def tile_painnmixing_pb_kernel(tc, h, mu_W, mu_VW, q, mu, W2_words, W2_scales, b
 
         h_sb = keep.tile([P, ATOM_TILES, K], BF16)
         h_rows = h.rearrange("(p a) o k -> p a (o k)", a=ATOM_TILES)
-        for half in range(2):
-            nc.sync.dma_start(out=h_sb[:, 2 * half : 2 * half + 2, :], in_=h_rows[:, 2 * half : 2 * half + 2, :])
+        for pair in range(ATOM_TILES // 2):
+            nc.sync.dma_start(out=h_sb[:, 2 * pair : 2 * pair + 2, :], in_=h_rows[:, 2 * pair : 2 * pair + 2, :])
 
         w_planes = keep.tile([P, PASSES, 3 * F], U8, align_bytes=64)
         nc.vector.memset(w_planes[:].bitcast(I32), 0)
@@ -76,14 +76,16 @@ def tile_painnmixing_pb_kernel(tc, h, mu_W, mu_VW, q, mu, W2_words, W2_scales, b
         mu_rows = mu.rearrange("(p a) c f -> p a c f", a=ATOM_TILES)
         w_words = {MU_BLOCK: load_words(MU_BLOCK)}
         muW_tiles, mu_tiles = [], []
-        for a in range(ATOM_TILES):
-            muW_a = inputs.tile([P, XYZ, F], BF16)
-            mu_a = inputs.tile([P, XYZ, F], BF16)
-            nc.sync.dma_start(out=muW_a[:], in_=muW_rows[:, a])
-            nc.sync.dma_start(out=mu_a[:], in_=mu_rows[:, a])
-            muW_tiles.append(muW_a)
-            mu_tiles.append(mu_a)
-            if a == 0:
+        for pair in range(ATOM_TILES // 2):
+            for a in (2 * pair, 2 * pair + 1):
+                muW_a = inputs.tile([P, XYZ, F], BF16)
+                nc.sync.dma_start(out=muW_a[:], in_=muW_rows[:, a])
+                muW_tiles.append(muW_a)
+            for a in (2 * pair, 2 * pair + 1):
+                mu_a = inputs.tile([P, XYZ, F], BF16)
+                nc.sync.dma_start(out=mu_a[:], in_=mu_rows[:, a])
+                mu_tiles.append(mu_a)
+            if pair == 0:
                 w_words[GATE_BLOCK] = load_words(GATE_BLOCK)
                 w_words[Q_BLOCK] = load_words(Q_BLOCK)
         gate_sb = keep.tile([P, ATOM_TILES, F], BF16)
@@ -96,7 +98,7 @@ def tile_painnmixing_pb_kernel(tc, h, mu_W, mu_VW, q, mu, W2_words, W2_scales, b
         nc.scalar.dma_start(out=bias_bf[:CHANNEL_TILES, :], in_=b2.rearrange("(j c) -> j c", c=P))
         bias_f32 = keep.tile([P, P], F32)
         nc.vector.tensor_copy(out=bias_f32[:], in_=bias_bf[:])
-        bias_turned = psum_acc.tile([P, P], F32, tag="acc")
+        bias_turned = psum.tile([P, P], F32, tag="bank")
         nc.tensor.transpose(bias_turned[:], bias_f32[:], ident[:])
         bias_col = keep.tile([P, CHANNEL_TILES], F32)
         nc.scalar.activation(out=bias_col[:], in_=bias_turned[:, :CHANNEL_TILES], func=IDENTITY)
@@ -104,18 +106,18 @@ def tile_painnmixing_pb_kernel(tc, h, mu_W, mu_VW, q, mu, W2_words, W2_scales, b
         h_codes = keep.tile([P, PASSES, ATOMS], U32, align_bytes=64)
         h_scales = keep.tile([P, PASSES, ATOMS], U8, align_bytes=64)
         h_words = h_sb[:].bitcast(F32)
-        for half in range(2):
-            atoms = slice(2 * P * half, 2 * P * (half + 1))
+        for pair in range(ATOM_TILES // 2):
+            atoms = slice(2 * P * pair, 2 * P * (pair + 1))
             for g in range(PASSES):
-                turned = psum_rows.tile([P, 2, 2 * P], F32, tag="x_rows")
+                turned = psum.tile([P, 2, 2 * P], F32, tag="bank")
                 for u in range(2):
                     for j in range(2):
                         nc.tensor.transpose(
                             turned[:, u, P * j : P * (j + 1)],
-                            h_words[:, 2 * half + j, WORDS_PER_PASS * g + u : WORDS_PER_PASS * (g + 1) : 2],
+                            h_words[:, 2 * pair + j, WORDS_PER_PASS * g + u : WORDS_PER_PASS * (g + 1) : 2],
                             ident[:],
                         )
-                grouped = keep.tile([P, 2 * P, 4], BF16, align_bytes=64, tag="grouped%d%d" % (half, g))
+                grouped = keep.tile([P, 2 * P, 4], BF16, align_bytes=64, tag="grouped%d%d" % (pair, g))
                 grouped_words = grouped[:].rearrange("p n t -> p (n t)").bitcast(F32).rearrange("p (n u) -> p n u", u=2)
                 if g == 0:
                     nc.scalar.copy(out=grouped_words, in_=turned[:].rearrange("p u n -> p n u"))
@@ -127,12 +129,14 @@ def tile_painnmixing_pb_kernel(tc, h, mu_W, mu_VW, q, mu, W2_words, W2_scales, b
                     in_=grouped[:].rearrange("p n t -> p (n t)"),
                 )
 
+        x_cols_of = {}
+
         def make_x_columns(block, half):
             x_cols = keep.tile([P, TILES_PER_BANK, ATOMS], F32, tag="x_cols%d%d" % (block, half))
             for i in range(TILES_PER_BANK):
                 in_block = TILES_PER_BANK * half + i
                 j = F // P * block + in_block
-                acc = psum_acc.tile([P, ATOMS], F32, tag="acc")
+                acc = psum.tile([P, ATOMS], F32, tag="bank")
                 for g in range(PASSES):
                     nc.tensor.matmul_mx(
                         out=acc[:],
@@ -144,53 +148,67 @@ def tile_painnmixing_pb_kernel(tc, h, mu_W, mu_VW, q, mu, W2_words, W2_scales, b
                         stop=(g == PASSES - 1),
                     )
                 nc.scalar.activation(out=x_cols[:, i, :], in_=acc[:], func=IDENTITY, bias=bias_col[:, j : j + 1])
-            return x_cols
+            x_cols_of[block, half] = x_cols
 
-        def turn_back(x_cols, a):
-            x_rows = psum_rows.tile([P, BANK], F32, tag="x_rows")
+        def turn_back(block, half, a, onto=None):
+            x_rows = psum.tile([P, BANK], F32, tag="bank")
+            if onto is not None:
+                nc.tensor.matmul(out=x_rows[:], lhsT=ident_bf[:], rhs=onto, start=True, stop=False)
             for i in range(TILES_PER_BANK):
-                nc.tensor.transpose(x_rows[:, P * i : P * (i + 1)], x_cols[:, i, P * a : P * (a + 1)], ident[:])
+                nc.tensor.matmul(
+                    out=x_rows[:, P * i : P * (i + 1)],
+                    lhsT=x_cols_of[block, half][:, i, P * a : P * (a + 1)],
+                    rhs=ident[:],
+                    is_transpose=True,
+                    start=(onto is None),
+                    stop=(onto is None or i == TILES_PER_BANK - 1),
+                )
             return x_rows
 
-        x_cols_of = {}
-        for half in range(HALVES):
-            x_cols_of[MU_BLOCK, half] = make_x_columns(MU_BLOCK, half)
+        x_order = [(block, half) for block in (MU_BLOCK, GATE_BLOCK, Q_BLOCK) for half in range(HALVES)]
+        make_x_columns(*x_order[0])
+        made = 1
+
         mu_out_rows = out_1.rearrange("(p a) c f -> p a c f", a=ATOM_TILES)
-        for a in range(ATOM_TILES):
-            mu_new = mu_results.tile([P, XYZ, F], F32)
+        for pair in range(ATOM_TILES // 2):
+            mu_new_of = {}
+            for a in (2 * pair, 2 * pair + 1):
+                mu_new = mu_results.tile([P, XYZ, F], F32)
+                mu_new_of[a] = mu_new
             for half in range(HALVES):
                 cols = slice(BANK * half, BANK * (half + 1))
-                x_mu = turn_back(x_cols_of[MU_BLOCK, half], a)
-                nc.vector.tensor_tensor(
-                    out=mu_new[:, :, cols],
-                    in0=x_mu[:].unsqueeze(1).to_broadcast([P, XYZ, BANK]),
-                    in1=muW_tiles[a][:, :, cols],
-                    op=MULT,
-                )
-                nc.gpsimd.tensor_tensor(out=mu_new[:, :, cols], in0=mu_new[:, :, cols], in1=mu_tiles[a][:, :, cols], op=ADD)
-                nc.sync.dma_start(out=mu_out_rows[:, a, :, cols], in_=mu_new[:, :, cols])
-            block = (GATE_BLOCK, Q_BLOCK)[a % 2]
-            x_cols_of[block, a // 2] = make_x_columns(block, a // 2)
+                for a in (2 * pair, 2 * pair + 1):
+                    x_mu = turn_back(MU_BLOCK, half, a)
+                    nc.vector.tensor_tensor(
+                        out=mu_new_of[a][:, :, cols],
+                        in0=x_mu[:].unsqueeze(1).to_broadcast([P, XYZ, BANK]),
+                        in1=muW_tiles[a][:, :, cols],
+                        op=MULT,
+                    )
+                for a in (2 * pair, 2 * pair + 1):
+                    if a == ATOM_TILES - 2 and half == HALVES - 1:
+                        for c in range(XYZ):
+                            mu_f32 = psum.tile([P, BANK], F32, tag="bank")
+                            nc.tensor.matmul(out=mu_f32[:], lhsT=ident_bf[:], rhs=mu_tiles[a][:, c, cols], start=True, stop=True)
+                            nc.vector.tensor_tensor(out=mu_new_of[a][:, c, cols], in0=mu_f32[:], in1=mu_new_of[a][:, c, cols], op=ADD)
+                    else:
+                        nc.gpsimd.tensor_tensor(
+                            out=mu_new_of[a][:, :, cols], in0=mu_new_of[a][:, :, cols], in1=mu_tiles[a][:, :, cols], op=ADD
+                        )
+                    nc.sync.dma_start(out=mu_out_rows[:, a, :, cols], in_=mu_new_of[a][:, :, cols])
+                make_x_columns(*x_order[made])
+                made += 1
+        make_x_columns(*x_order[made])
 
         q_out_rows = out_0.rearrange("(p a) o f -> p a (o f)", a=ATOM_TILES)
         for a in range(ATOM_TILES):
             q_new = q_results.tile([P, F], F32)
             for half in range(HALVES):
                 cols = slice(BANK * half, BANK * (half + 1))
-                x_gate = turn_back(x_cols_of[GATE_BLOCK, half], a)
+                x_gate = turn_back(GATE_BLOCK, half, a)
                 nc.vector.tensor_tensor(out=q_new[:, cols], in0=x_gate[:], in1=gate_sb[:, a, cols], op=MULT)
             for half in range(HALVES):
                 cols = slice(BANK * half, BANK * (half + 1))
-                q_plus_x = psum_rows.tile([P, BANK], F32, tag="x_rows")
-                nc.tensor.matmul(out=q_plus_x[:], lhsT=ident_bf[:], rhs=q_sb[:, a, cols], start=True, stop=False)
-                for i in range(TILES_PER_BANK):
-                    nc.tensor.matmul(
-                        out=q_plus_x[:, P * i : P * (i + 1)],
-                        lhsT=x_cols_of[Q_BLOCK, half][:, i, P * a : P * (a + 1)],
-                        rhs=ident[:],
-                        is_transpose=True,
-                        start=False,
-                        stop=(i == TILES_PER_BANK - 1),
-                    )
+                q_plus_x = turn_back(Q_BLOCK, half, a, onto=q_sb[:, a, cols])
                 nc.vector.tensor_tensor(out=q_new[:, cols], in0=q_plus_x[:], in1=q_new[:, cols], op=ADD)
             nc.scalar.dma_start(out=q_out_rows[:, a], in_=q_new[:])

@@ -39,7 +39,7 @@ def tile_painnmixing_pb_kernel(tc, h, mu_W, mu_VW, q, mu, W2_words, W2_scales, b
     nc = tc.nc
     with ExitStack() as ctx:
         keep = ctx.enter_context(tc.tile_pool(name="keep", bufs=1))
-        inputs = ctx.enter_context(tc.tile_pool(name="inputs", bufs=ATOM_TILES))
+        inputs = ctx.enter_context(tc.tile_pool(name="inputs", bufs=ATOM_TILES // 2))
         mu_results = ctx.enter_context(tc.tile_pool(name="mu_results", bufs=ATOM_TILES))
         q_results = ctx.enter_context(tc.tile_pool(name="q_results", bufs=2))
         psum = ctx.enter_context(tc.psum_pool(name="psum", bufs=PSUM_BANKS))
@@ -58,12 +58,8 @@ def tile_painnmixing_pb_kernel(tc, h, mu_W, mu_VW, q, mu, W2_words, W2_scales, b
         w_planes = keep.tile([P, PASSES, 3 * F], U8, align_bytes=64)
         nc.vector.memset(w_planes[:].bitcast(I32), 0)
         scale_rows = W2_scales.rearrange("g r n -> r g n")
-        for low_q in range(2):
-            for i in range(4):
-                nc.sync.dma_start(
-                    out=w_planes[32 * low_q + i : P : 64].bitcast(I32),
-                    in_=scale_rows[4 * low_q + i : 16 : 8].bitcast(I32),
-                )
+        for i in range(4):
+            nc.sync.dma_start(out=w_planes[i : P : 32].bitcast(I32), in_=scale_rows[i : 16 : 4].bitcast(I32))
 
         word_rows = W2_words.rearrange("g p b -> p g b")
 
@@ -77,14 +73,13 @@ def tile_painnmixing_pb_kernel(tc, h, mu_W, mu_VW, q, mu, W2_words, W2_scales, b
         w_words = {MU_BLOCK: load_words(MU_BLOCK)}
         muW_tiles, mu_tiles = [], []
         for pair in range(ATOM_TILES // 2):
-            for a in (2 * pair, 2 * pair + 1):
-                muW_a = inputs.tile([P, XYZ, F], BF16)
-                nc.sync.dma_start(out=muW_a[:], in_=muW_rows[:, a])
-                muW_tiles.append(muW_a)
-            for a in (2 * pair, 2 * pair + 1):
-                mu_a = inputs.tile([P, XYZ, F], BF16)
-                nc.sync.dma_start(out=mu_a[:], in_=mu_rows[:, a])
-                mu_tiles.append(mu_a)
+            muW_pair = inputs.tile([P, 2, XYZ, F], BF16)
+            mu_pair = inputs.tile([P, 2, XYZ, F], BF16)
+            nc.sync.dma_start(out=muW_pair[:], in_=muW_rows[:, 2 * pair : 2 * pair + 2])
+            nc.sync.dma_start(out=mu_pair[:], in_=mu_rows[:, 2 * pair : 2 * pair + 2])
+            for j in range(2):
+                muW_tiles.append(muW_pair[:, j])
+                mu_tiles.append(mu_pair[:, j])
             if pair == 0:
                 w_words[GATE_BLOCK] = load_words(GATE_BLOCK)
                 w_words[Q_BLOCK] = load_words(Q_BLOCK)
@@ -186,7 +181,7 @@ def tile_painnmixing_pb_kernel(tc, h, mu_W, mu_VW, q, mu, W2_words, W2_scales, b
                         op=MULT,
                     )
                 for a in (2 * pair, 2 * pair + 1):
-                    if a == ATOM_TILES - 2 and half == HALVES - 1:
+                    if a == ATOM_TILES - 1 and half == 0:
                         for c in range(XYZ):
                             mu_f32 = psum.tile([P, BANK], F32, tag="bank")
                             nc.tensor.matmul(out=mu_f32[:], lhsT=ident_bf[:], rhs=mu_tiles[a][:, c, cols], start=True, stop=True)
@@ -195,7 +190,10 @@ def tile_painnmixing_pb_kernel(tc, h, mu_W, mu_VW, q, mu, W2_words, W2_scales, b
                         nc.gpsimd.tensor_tensor(
                             out=mu_new_of[a][:, :, cols], in0=mu_new_of[a][:, :, cols], in1=mu_tiles[a][:, :, cols], op=ADD
                         )
-                    nc.sync.dma_start(out=mu_out_rows[:, a, :, cols], in_=mu_new_of[a][:, :, cols])
+                    if a == ATOM_TILES - 1:
+                        nc.sync.dma_start(out=mu_out_rows[:, a, :, cols], in_=mu_new_of[a][:, :, cols])
+                    elif half == HALVES - 1:
+                        nc.sync.dma_start(out=mu_out_rows[:, a], in_=mu_new_of[a][:])
                 make_x_columns(*x_order[made])
                 made += 1
         make_x_columns(*x_order[made])

@@ -31,6 +31,7 @@ PSUM_BANKS = 8
 HALVES = F // BANK
 CHANNEL_TILES = 3 * F // P
 TILES_PER_BANK = BANK // P
+VECTOR_SUMS = 1
 
 FLOPS = 2 * ATOMS * K * 3 * F
 
@@ -39,9 +40,9 @@ def tile_painnmixing_pb_kernel(tc, h, mu_W, mu_VW, q, mu, W2_words, W2_scales, b
     nc = tc.nc
     with ExitStack() as ctx:
         keep = ctx.enter_context(tc.tile_pool(name="keep", bufs=1))
-        inputs = ctx.enter_context(tc.tile_pool(name="inputs", bufs=ATOM_TILES // 2))
+        inputs = ctx.enter_context(tc.tile_pool(name="inputs", bufs=ATOM_TILES))
         mu_results = ctx.enter_context(tc.tile_pool(name="mu_results", bufs=ATOM_TILES))
-        q_results = ctx.enter_context(tc.tile_pool(name="q_results", bufs=2))
+        q_results = ctx.enter_context(tc.tile_pool(name="q_results", bufs=ATOM_TILES))
         psum = ctx.enter_context(tc.psum_pool(name="psum", bufs=PSUM_BANKS))
         ctx.enter_context(tc.manual_schedule())
 
@@ -58,8 +59,12 @@ def tile_painnmixing_pb_kernel(tc, h, mu_W, mu_VW, q, mu, W2_words, W2_scales, b
         w_planes = keep.tile([P, PASSES, 3 * F], U8, align_bytes=64)
         nc.vector.memset(w_planes[:].bitcast(I32), 0)
         scale_rows = W2_scales.rearrange("g r n -> r g n")
-        for i in range(4):
-            nc.sync.dma_start(out=w_planes[i : P : 32].bitcast(I32), in_=scale_rows[i : 16 : 4].bitcast(I32))
+        for low_q in range(2):
+            for i in range(4):
+                nc.sync.dma_start(
+                    out=w_planes[32 * low_q + i : P : 64].bitcast(I32),
+                    in_=scale_rows[4 * low_q + i : 16 : 8].bitcast(I32),
+                )
 
         word_rows = W2_words.rearrange("g p b -> p g b")
 
@@ -73,13 +78,14 @@ def tile_painnmixing_pb_kernel(tc, h, mu_W, mu_VW, q, mu, W2_words, W2_scales, b
         w_words = {MU_BLOCK: load_words(MU_BLOCK)}
         muW_tiles, mu_tiles = [], []
         for pair in range(ATOM_TILES // 2):
-            muW_pair = inputs.tile([P, 2, XYZ, F], BF16)
-            mu_pair = inputs.tile([P, 2, XYZ, F], BF16)
-            nc.sync.dma_start(out=muW_pair[:], in_=muW_rows[:, 2 * pair : 2 * pair + 2])
-            nc.sync.dma_start(out=mu_pair[:], in_=mu_rows[:, 2 * pair : 2 * pair + 2])
-            for j in range(2):
-                muW_tiles.append(muW_pair[:, j])
-                mu_tiles.append(mu_pair[:, j])
+            for a in (2 * pair, 2 * pair + 1):
+                muW_a = inputs.tile([P, XYZ, F], BF16)
+                nc.sync.dma_start(out=muW_a[:], in_=muW_rows[:, a])
+                muW_tiles.append(muW_a)
+            for a in (2 * pair, 2 * pair + 1):
+                mu_a = inputs.tile([P, XYZ, F], BF16)
+                nc.sync.dma_start(out=mu_a[:], in_=mu_rows[:, a])
+                mu_tiles.append(mu_a)
             if pair == 0:
                 w_words[GATE_BLOCK] = load_words(GATE_BLOCK)
                 w_words[Q_BLOCK] = load_words(Q_BLOCK)
@@ -126,23 +132,30 @@ def tile_painnmixing_pb_kernel(tc, h, mu_W, mu_VW, q, mu, W2_words, W2_scales, b
 
         x_cols_of = {}
 
-        def make_x_columns(block, half):
+        def make_x_columns(block, half, vector_helps=False):
             x_cols = keep.tile([P, TILES_PER_BANK, ATOMS], F32, tag="x_cols%d%d" % (block, half))
+            first_tile = TILES_PER_BANK * half
+            accs = []
             for i in range(TILES_PER_BANK):
-                in_block = TILES_PER_BANK * half + i
-                j = F // P * block + in_block
                 acc = psum.tile([P, ATOMS], F32, tag="bank")
-                for g in range(PASSES):
+                accs.append(acc)
+            for g in range(PASSES):
+                for i in range(TILES_PER_BANK):
                     nc.tensor.matmul_mx(
-                        out=acc[:],
-                        lhsT=w_words[block][:, g, 2 * P * in_block : 2 * P * (in_block + 1)].bitcast(FP4X4),
-                        lhsT_scale=w_planes[:, g, P * j : P * (j + 1)],
+                        out=accs[i][:],
+                        lhsT=w_words[block][:, g, 2 * P * (first_tile + i) : 2 * P * (first_tile + i + 1)].bitcast(FP4X4),
+                        lhsT_scale=w_planes[:, g, F * block + P * (first_tile + i) : F * block + P * (first_tile + i + 1)],
                         rhs=h_codes[:, g, :].bitcast(FP8X4),
                         rhs_scale=h_scales[:, g, :],
                         start=(g == 0),
                         stop=(g == PASSES - 1),
                     )
-                nc.scalar.activation(out=x_cols[:, i, :], in_=acc[:], func=IDENTITY, bias=bias_col[:, j : j + 1])
+            for i in range(TILES_PER_BANK):
+                j = F // P * block + first_tile + i
+                if vector_helps and i % 2 == 1:
+                    nc.vector.tensor_scalar(out=x_cols[:, i, :], in0=accs[i][:], scalar1=bias_col[:, j : j + 1], scalar2=None, op0=ADD)
+                else:
+                    nc.scalar.activation(out=x_cols[:, i, :], in_=accs[i][:], func=IDENTITY, bias=bias_col[:, j : j + 1])
             x_cols_of[block, half] = x_cols
 
         def turn_back(block, half, a, onto=None):
@@ -161,7 +174,7 @@ def tile_painnmixing_pb_kernel(tc, h, mu_W, mu_VW, q, mu, W2_words, W2_scales, b
             return x_rows
 
         x_order = [(block, half) for block in (MU_BLOCK, GATE_BLOCK, Q_BLOCK) for half in range(HALVES)]
-        make_x_columns(*x_order[0])
+        make_x_columns(*x_order[0], vector_helps=True)
         made = 1
 
         mu_out_rows = out_1.rearrange("(p a) c f -> p a c f", a=ATOM_TILES)
@@ -181,19 +194,19 @@ def tile_painnmixing_pb_kernel(tc, h, mu_W, mu_VW, q, mu, W2_words, W2_scales, b
                         op=MULT,
                     )
                 for a in (2 * pair, 2 * pair + 1):
-                    if a == ATOM_TILES - 1 and half == 0:
-                        for c in range(XYZ):
-                            mu_f32 = psum.tile([P, BANK], F32, tag="bank")
-                            nc.tensor.matmul(out=mu_f32[:], lhsT=ident_bf[:], rhs=mu_tiles[a][:, c, cols], start=True, stop=True)
-                            nc.vector.tensor_tensor(out=mu_new_of[a][:, c, cols], in0=mu_f32[:], in1=mu_new_of[a][:, c, cols], op=ADD)
-                    else:
-                        nc.gpsimd.tensor_tensor(
-                            out=mu_new_of[a][:, :, cols], in0=mu_new_of[a][:, :, cols], in1=mu_tiles[a][:, :, cols], op=ADD
-                        )
-                    if a == ATOM_TILES - 1:
-                        nc.sync.dma_start(out=mu_out_rows[:, a, :, cols], in_=mu_new_of[a][:, :, cols])
-                    elif half == HALVES - 1:
-                        nc.sync.dma_start(out=mu_out_rows[:, a], in_=mu_new_of[a][:])
+                    last = a == ATOM_TILES - 1 and half == HALVES - 1
+                    on_gpsimd = XYZ - VECTOR_SUMS if last else XYZ
+                    nc.gpsimd.tensor_tensor(
+                        out=mu_new_of[a][:, :on_gpsimd, cols],
+                        in0=mu_new_of[a][:, :on_gpsimd, cols],
+                        in1=mu_tiles[a][:, :on_gpsimd, cols],
+                        op=ADD,
+                    )
+                    for c in range(on_gpsimd, XYZ):
+                        mu_f32 = psum.tile([P, BANK], F32, tag="bank")
+                        nc.tensor.matmul(out=mu_f32[:], lhsT=ident_bf[:], rhs=mu_tiles[a][:, c, cols], start=True, stop=True)
+                        nc.vector.tensor_tensor(out=mu_new_of[a][:, c, cols], in0=mu_f32[:], in1=mu_new_of[a][:, c, cols], op=ADD)
+                    nc.sync.dma_start(out=mu_out_rows[:, a, :, cols], in_=mu_new_of[a][:, :, cols])
                 make_x_columns(*x_order[made])
                 made += 1
         make_x_columns(*x_order[made])
@@ -209,4 +222,4 @@ def tile_painnmixing_pb_kernel(tc, h, mu_W, mu_VW, q, mu, W2_words, W2_scales, b
                 cols = slice(BANK * half, BANK * (half + 1))
                 q_plus_x = turn_back(Q_BLOCK, half, a, onto=q_sb[:, a, cols])
                 nc.vector.tensor_tensor(out=q_new[:, cols], in0=q_plus_x[:], in1=q_new[:, cols], op=ADD)
-            nc.scalar.dma_start(out=q_out_rows[:, a], in_=q_new[:])
+                nc.scalar.dma_start(out=q_out_rows[:, a, cols], in_=q_new[:, cols])

@@ -51,6 +51,10 @@ def tile_painnmixing_pb_kernel(tc, h, mu_W, mu_VW, q, mu, W2_words, W2_scales, b
         ident_bf = keep.tile([P, P], BF16)
         make_identity(nc, ident_bf[:])
 
+        bias_bf = keep.tile([P, P], BF16)
+        nc.vector.memset(bias_bf[:], 0.0)
+        nc.scalar.dma_start(out=bias_bf[:CHANNEL_TILES, :], in_=b2.rearrange("(j c) -> j c", c=P))
+
         h_sb = keep.tile([P, ATOM_TILES, K], BF16)
         h_rows = h.rearrange("(p a) o k -> p a (o k)", a=ATOM_TILES)
         for pair in range(ATOM_TILES // 2):
@@ -94,16 +98,6 @@ def tile_painnmixing_pb_kernel(tc, h, mu_W, mu_VW, q, mu, W2_words, W2_scales, b
         nc.sync.dma_start(out=gate_sb[:], in_=mu_VW.rearrange("(p a) o f -> p a (o f)", a=ATOM_TILES))
         nc.sync.dma_start(out=q_sb[:], in_=q.rearrange("(p a) o f -> p a (o f)", a=ATOM_TILES))
 
-        bias_bf = keep.tile([P, P], BF16)
-        nc.vector.memset(bias_bf[:], 0.0)
-        nc.scalar.dma_start(out=bias_bf[:CHANNEL_TILES, :], in_=b2.rearrange("(j c) -> j c", c=P))
-        bias_f32 = keep.tile([P, P], F32)
-        nc.vector.tensor_copy(out=bias_f32[:], in_=bias_bf[:])
-        bias_turned = psum.tile([P, P], F32, tag="bank")
-        nc.tensor.transpose(bias_turned[:], bias_f32[:], ident[:])
-        bias_col = keep.tile([P, CHANNEL_TILES], F32)
-        nc.scalar.activation(out=bias_col[:], in_=bias_turned[:, :CHANNEL_TILES], func=IDENTITY)
-
         h_codes = keep.tile([P, PASSES, ATOMS], U32, align_bytes=64)
         h_scales = keep.tile([P, PASSES, ATOMS], U8, align_bytes=64)
         h_words = h_sb[:].bitcast(F32)
@@ -129,6 +123,11 @@ def tile_painnmixing_pb_kernel(tc, h, mu_W, mu_VW, q, mu, W2_words, W2_scales, b
                     scales=h_scales[:, g, atoms],
                     in_=grouped[:].rearrange("p n t -> p (n t)"),
                 )
+
+        bias_turned = psum.tile([P, P], BF16, tag="bank")
+        nc.tensor.transpose(bias_turned[:], bias_bf[:], ident_bf[:])
+        bias_col = keep.tile([P, CHANNEL_TILES], F32)
+        nc.scalar.activation(out=bias_col[:], in_=bias_turned[:, :CHANNEL_TILES], func=IDENTITY)
 
         x_cols_of = {}
 

@@ -51,48 +51,50 @@ def tile_painnmixing_pb_kernel(tc, h, mu_W, mu_VW, q, mu, W2_words, W2_scales, b
         ident_bf = keep.tile([P, P], BF16)
         make_identity(nc, ident_bf[:])
 
-        bias_bf = keep.tile([P, P], BF16)
-        nc.vector.memset(bias_bf[:], 0.0)
-        nc.scalar.dma_start(out=bias_bf[:CHANNEL_TILES, :], in_=b2.rearrange("(j c) -> j c", c=P))
-
         h_sb = keep.tile([P, ATOM_TILES, K], BF16)
         h_rows = h.rearrange("(p a) o k -> p a (o k)", a=ATOM_TILES)
         for pair in range(ATOM_TILES // 2):
             nc.sync.dma_start(out=h_sb[:, 2 * pair : 2 * pair + 2, :], in_=h_rows[:, 2 * pair : 2 * pair + 2, :])
 
-        w_planes = keep.tile([P, PASSES, 3 * F], U8, align_bytes=64)
-        nc.vector.memset(w_planes[:].bitcast(I32), 0)
-        scale_rows = W2_scales.rearrange("g r n -> r g n")
-        for low_q in range(2):
-            for i in range(4):
-                nc.sync.dma_start(
-                    out=w_planes[32 * low_q + i : P : 64].bitcast(I32),
-                    in_=scale_rows[4 * low_q + i : 16 : 8].bitcast(I32),
-                )
+        w_planes = {}
+        bias_bf = keep.tile([P, P], BF16)
+        for block in (MU_BLOCK, GATE_BLOCK, Q_BLOCK):
+            planes = keep.tile([P, PASSES, F], U8, align_bytes=64, tag="planes%d" % block)
+            nc.vector.memset(planes[:].bitcast(I32), 0)
+            w_planes[block] = planes
+            if block == MU_BLOCK:
+                nc.vector.memset(bias_bf[:], 0.0)
+        nc.scalar.dma_start(out=bias_bf[:CHANNEL_TILES, :], in_=b2.rearrange("(j c) -> j c", c=P))
 
         word_rows = W2_words.rearrange("g p b -> p g b")
+        scale_rows = W2_scales.rearrange("g r n -> r g n")
+        w_words = {}
 
-        def load_words(block):
+        def load_weight(block):
             words = keep.tile([P, PASSES, 2 * F], U8, align_bytes=64, tag="words%d" % block)
             nc.sync.dma_start(out=words[:].bitcast(I32), in_=word_rows[:, :, 2 * F * block : 2 * F * (block + 1)].bitcast(I32))
-            return words
+            w_words[block] = words
+            for i in range(4):
+                nc.sync.dma_start(
+                    out=w_planes[block][i:P:32].bitcast(I32),
+                    in_=scale_rows[i:16:4, :, F * block : F * (block + 1)].bitcast(I32),
+                )
 
         muW_rows = mu_W.rearrange("(p a) c f -> p a c f", a=ATOM_TILES)
         mu_rows = mu.rearrange("(p a) c f -> p a c f", a=ATOM_TILES)
-        w_words = {MU_BLOCK: load_words(MU_BLOCK)}
+        load_weight(MU_BLOCK)
         muW_tiles, mu_tiles = [], []
-        for pair in range(ATOM_TILES // 2):
-            for a in (2 * pair, 2 * pair + 1):
-                muW_a = inputs.tile([P, XYZ, F], BF16)
-                nc.sync.dma_start(out=muW_a[:], in_=muW_rows[:, a])
-                muW_tiles.append(muW_a)
-            for a in (2 * pair, 2 * pair + 1):
-                mu_a = inputs.tile([P, XYZ, F], BF16)
-                nc.sync.dma_start(out=mu_a[:], in_=mu_rows[:, a])
-                mu_tiles.append(mu_a)
-            if pair == 0:
-                w_words[GATE_BLOCK] = load_words(GATE_BLOCK)
-                w_words[Q_BLOCK] = load_words(Q_BLOCK)
+        for a in range(ATOM_TILES):
+            muW_a = inputs.tile([P, XYZ, F], BF16)
+            nc.sync.dma_start(out=muW_a[:], in_=muW_rows[:, a])
+            muW_tiles.append(muW_a)
+            mu_a = inputs.tile([P, XYZ, F], BF16)
+            nc.sync.dma_start(out=mu_a[:], in_=mu_rows[:, a])
+            mu_tiles.append(mu_a)
+            if a == 1:
+                load_weight(GATE_BLOCK)
+            if a == 2:
+                load_weight(Q_BLOCK)
         gate_sb = keep.tile([P, ATOM_TILES, F], BF16)
         q_sb = keep.tile([P, ATOM_TILES, F], BF16)
         nc.sync.dma_start(out=gate_sb[:], in_=mu_VW.rearrange("(p a) o f -> p a (o f)", a=ATOM_TILES))
@@ -143,7 +145,7 @@ def tile_painnmixing_pb_kernel(tc, h, mu_W, mu_VW, q, mu, W2_words, W2_scales, b
                     nc.tensor.matmul_mx(
                         out=accs[i][:],
                         lhsT=w_words[block][:, g, 2 * P * (first_tile + i) : 2 * P * (first_tile + i + 1)].bitcast(FP4X4),
-                        lhsT_scale=w_planes[:, g, F * block + P * (first_tile + i) : F * block + P * (first_tile + i + 1)],
+                        lhsT_scale=w_planes[block][:, g, P * (first_tile + i) : P * (first_tile + i + 1)],
                         rhs=h_codes[:, g, :].bitcast(FP8X4),
                         rhs_scale=h_scales[:, g, :],
                         start=(g == 0),

@@ -31,7 +31,8 @@ PSUM_BANKS = 8
 HALVES = F // BANK
 CHANNEL_TILES = 3 * F // P
 TILES_PER_BANK = BANK // P
-VECTOR_SUMS = 1
+VECTOR_HALF_TILES = ((2, 1), (3, 1))
+SUMS_A_STEP = 2
 
 FLOPS = 2 * ATOMS * K * 3 * F
 
@@ -175,12 +176,13 @@ def tile_painnmixing_pb_kernel(tc, h, mu_W, mu_VW, q, mu, W2_words, W2_scales, b
             return x_rows
 
         x_order = [(block, half) for block in (MU_BLOCK, GATE_BLOCK, Q_BLOCK) for half in range(HALVES)]
+        made_behind = {(0, 0): 1, (0, 1): 1, (1, 0): 2, (1, 1): 1}
         make_x_columns(*x_order[0], vector_helps=True)
         made = 1
 
         mu_out_rows = out_1.rearrange("(p a) c f -> p a c f", a=ATOM_TILES)
+        mu_new_of = {}
         for pair in range(ATOM_TILES // 2):
-            mu_new_of = {}
             for a in (2 * pair, 2 * pair + 1):
                 mu_new = mu_results.tile([P, XYZ, F], F32)
                 mu_new_of[a] = mu_new
@@ -195,25 +197,26 @@ def tile_painnmixing_pb_kernel(tc, h, mu_W, mu_VW, q, mu, W2_words, W2_scales, b
                         op=MULT,
                     )
                 for a in (2 * pair, 2 * pair + 1):
-                    last = a == ATOM_TILES - 1 and half == HALVES - 1
-                    on_gpsimd = XYZ - VECTOR_SUMS if last else XYZ
-                    nc.gpsimd.tensor_tensor(
-                        out=mu_new_of[a][:, :on_gpsimd, cols],
-                        in0=mu_new_of[a][:, :on_gpsimd, cols],
-                        in1=mu_tiles[a][:, :on_gpsimd, cols],
-                        op=ADD,
-                    )
-                    for c in range(on_gpsimd, XYZ):
-                        mu_f32 = psum.tile([P, BANK], F32, tag="bank")
-                        nc.tensor.matmul(out=mu_f32[:], lhsT=ident_bf[:], rhs=mu_tiles[a][:, c, cols], start=True, stop=True)
-                        nc.vector.tensor_tensor(out=mu_new_of[a][:, c, cols], in0=mu_f32[:], in1=mu_new_of[a][:, c, cols], op=ADD)
-                    nc.sync.dma_start(out=mu_out_rows[:, a, :, cols], in_=mu_new_of[a][:, :, cols])
-                make_x_columns(*x_order[made])
-                made += 1
-        make_x_columns(*x_order[made])
+                    if (a, half) not in VECTOR_HALF_TILES:
+                        nc.gpsimd.tensor_tensor(out=mu_new_of[a][:, :, cols], in0=mu_new_of[a][:, :, cols], in1=mu_tiles[a][:, :, cols], op=ADD)
+                        nc.sync.dma_start(out=mu_out_rows[:, a, :, cols], in_=mu_new_of[a][:, :, cols])
+                for n in range(made_behind[pair, half]):
+                    make_x_columns(*x_order[made])
+                    made += 1
 
+        def vector_sum(a, half, c):
+            cols = slice(BANK * half, BANK * (half + 1))
+            mu_f32 = psum.tile([P, BANK], F32, tag="bank")
+            nc.tensor.matmul(out=mu_f32[:], lhsT=ident_bf[:], rhs=mu_tiles[a][:, c, cols], start=True, stop=True)
+            nc.vector.tensor_tensor(out=mu_new_of[a][:, c, cols], in0=mu_f32[:], in1=mu_new_of[a][:, c, cols], op=ADD)
+            if c == XYZ - 1:
+                nc.scalar.dma_start(out=mu_out_rows[:, a, :, cols], in_=mu_new_of[a][:, :, cols])
+
+        vector_sums = [(a, half, c) for (a, half) in VECTOR_HALF_TILES for c in range(XYZ)]
         q_out_rows = out_0.rearrange("(p a) o f -> p a (o f)", a=ATOM_TILES)
         for a in range(ATOM_TILES):
+            for job in vector_sums[SUMS_A_STEP * a : SUMS_A_STEP * (a + 1)]:
+                vector_sum(*job)
             q_new = q_results.tile([P, F], F32)
             for half in range(HALVES):
                 cols = slice(BANK * half, BANK * (half + 1))

@@ -33,6 +33,7 @@ CHANNEL_TILES = 3 * F // P
 TILES_PER_BANK = BANK // P
 VECTOR_HALF_TILES = ((2, 1), (3, 1))
 SUMS_A_STEP = 2
+SINGLE_TILES = 2
 
 FLOPS = 2 * ATOMS * K * 3 * F
 
@@ -41,9 +42,8 @@ def tile_painnmixing_pb_kernel(tc, h, mu_W, mu_VW, q, mu, W2_words, W2_scales, b
     nc = tc.nc
     with ExitStack() as ctx:
         keep = ctx.enter_context(tc.tile_pool(name="keep", bufs=1))
-        inputs = ctx.enter_context(tc.tile_pool(name="inputs", bufs=ATOM_TILES))
-        mu_results = ctx.enter_context(tc.tile_pool(name="mu_results", bufs=ATOM_TILES))
-        q_results = ctx.enter_context(tc.tile_pool(name="q_results", bufs=ATOM_TILES))
+        inputs = ctx.enter_context(tc.tile_pool(name="inputs", bufs=SINGLE_TILES))
+        mu_results = ctx.enter_context(tc.tile_pool(name="mu_results", bufs=2))
         psum = ctx.enter_context(tc.psum_pool(name="psum", bufs=PSUM_BANKS))
         ctx.enter_context(tc.manual_schedule())
 
@@ -57,45 +57,44 @@ def tile_painnmixing_pb_kernel(tc, h, mu_W, mu_VW, q, mu, W2_words, W2_scales, b
         for pair in range(ATOM_TILES // 2):
             nc.sync.dma_start(out=h_sb[:, 2 * pair : 2 * pair + 2, :], in_=h_rows[:, 2 * pair : 2 * pair + 2, :])
 
-        w_planes = {}
+        w_planes = keep.tile([P, PASSES, 3 * F], U8, align_bytes=64)
+        nc.vector.memset(w_planes[:].bitcast(I32), 0)
         bias_bf = keep.tile([P, P], BF16)
-        for block in (MU_BLOCK, GATE_BLOCK, Q_BLOCK):
-            planes = keep.tile([P, PASSES, F], U8, align_bytes=64, tag="planes%d" % block)
-            nc.vector.memset(planes[:].bitcast(I32), 0)
-            w_planes[block] = planes
-            if block == MU_BLOCK:
-                nc.vector.memset(bias_bf[:], 0.0)
+        nc.vector.memset(bias_bf[:], 0.0)
         nc.scalar.dma_start(out=bias_bf[:CHANNEL_TILES, :], in_=b2.rearrange("(j c) -> j c", c=P))
 
         word_rows = W2_words.rearrange("g p b -> p g b")
         scale_rows = W2_scales.rearrange("g r n -> r g n")
         w_words = {}
 
-        def load_weight(block):
+        def load_words(block):
             words = keep.tile([P, PASSES, 2 * F], U8, align_bytes=64, tag="words%d" % block)
             nc.sync.dma_start(out=words[:].bitcast(I32), in_=word_rows[:, :, 2 * F * block : 2 * F * (block + 1)].bitcast(I32))
             w_words[block] = words
-            for i in range(4):
-                nc.sync.dma_start(
-                    out=w_planes[block][i:P:32].bitcast(I32),
-                    in_=scale_rows[i:16:4, :, F * block : F * (block + 1)].bitcast(I32),
-                )
+
+        load_words(MU_BLOCK)
+        for i in range(4):
+            nc.sync.dma_start(out=w_planes[i:P:32].bitcast(I32), in_=scale_rows[i:16:4].bitcast(I32))
 
         muW_rows = mu_W.rearrange("(p a) c f -> p a c f", a=ATOM_TILES)
         mu_rows = mu.rearrange("(p a) c f -> p a c f", a=ATOM_TILES)
-        load_weight(MU_BLOCK)
-        muW_tiles, mu_tiles = [], []
-        for a in range(ATOM_TILES):
+        muW_of, mu_of = {}, {}
+        for a in range(SINGLE_TILES):
             muW_a = inputs.tile([P, XYZ, F], BF16)
             nc.sync.dma_start(out=muW_a[:], in_=muW_rows[:, a])
-            muW_tiles.append(muW_a)
+            muW_of[a] = muW_a[:]
             mu_a = inputs.tile([P, XYZ, F], BF16)
             nc.sync.dma_start(out=mu_a[:], in_=mu_rows[:, a])
-            mu_tiles.append(mu_a)
-            if a == 1:
-                load_weight(GATE_BLOCK)
-            if a == 2:
-                load_weight(Q_BLOCK)
+            mu_of[a] = mu_a[:]
+        load_words(GATE_BLOCK)
+        muW_rest = keep.tile([P, ATOM_TILES - SINGLE_TILES, XYZ, F], BF16)
+        nc.sync.dma_start(out=muW_rest[:], in_=muW_rows[:, SINGLE_TILES:])
+        load_words(Q_BLOCK)
+        mu_rest = keep.tile([P, ATOM_TILES - SINGLE_TILES, XYZ, F], BF16)
+        nc.sync.dma_start(out=mu_rest[:], in_=mu_rows[:, SINGLE_TILES:])
+        for a in range(SINGLE_TILES, ATOM_TILES):
+            muW_of[a] = muW_rest[:, a - SINGLE_TILES]
+            mu_of[a] = mu_rest[:, a - SINGLE_TILES]
         gate_sb = keep.tile([P, ATOM_TILES, F], BF16)
         q_sb = keep.tile([P, ATOM_TILES, F], BF16)
         nc.sync.dma_start(out=gate_sb[:], in_=mu_VW.rearrange("(p a) o f -> p a (o f)", a=ATOM_TILES))
@@ -146,7 +145,7 @@ def tile_painnmixing_pb_kernel(tc, h, mu_W, mu_VW, q, mu, W2_words, W2_scales, b
                     nc.tensor.matmul_mx(
                         out=accs[i][:],
                         lhsT=w_words[block][:, g, 2 * P * (first_tile + i) : 2 * P * (first_tile + i + 1)].bitcast(FP4X4),
-                        lhsT_scale=w_planes[block][:, g, P * (first_tile + i) : P * (first_tile + i + 1)],
+                        lhsT_scale=w_planes[:, g, F * block + P * (first_tile + i) : F * block + P * (first_tile + i + 1)],
                         rhs=h_codes[:, g, :].bitcast(FP8X4),
                         rhs_scale=h_scales[:, g, :],
                         start=(g == 0),
@@ -176,54 +175,78 @@ def tile_painnmixing_pb_kernel(tc, h, mu_W, mu_VW, q, mu, W2_words, W2_scales, b
             return x_rows
 
         x_order = [(block, half) for block in (MU_BLOCK, GATE_BLOCK, Q_BLOCK) for half in range(HALVES)]
-        made_behind = {(0, 0): 1, (0, 1): 1, (1, 0): 2, (1, 1): 1}
         make_x_columns(*x_order[0], vector_helps=True)
-        made = 1
 
         mu_out_rows = out_1.rearrange("(p a) c f -> p a c f", a=ATOM_TILES)
-        mu_new_of = {}
-        for pair in range(ATOM_TILES // 2):
-            for a in (2 * pair, 2 * pair + 1):
-                mu_new = mu_results.tile([P, XYZ, F], F32)
-                mu_new_of[a] = mu_new
-            for half in range(HALVES):
-                cols = slice(BANK * half, BANK * (half + 1))
-                for a in (2 * pair, 2 * pair + 1):
-                    x_mu = turn_back(MU_BLOCK, half, a)
-                    nc.vector.tensor_tensor(
-                        out=mu_new_of[a][:, :, cols],
-                        in0=x_mu[:].unsqueeze(1).to_broadcast([P, XYZ, BANK]),
-                        in1=muW_tiles[a][:, :, cols],
-                        op=MULT,
+        mu_new_01 = keep.tile([P, 2, XYZ, F], F32)
+        mu_new_of = {0: mu_new_01[:, 0], 1: mu_new_01[:, 1]}
+        for a in (2, 3):
+            mu_new = mu_results.tile([P, XYZ, F], F32)
+            mu_new_of[a] = mu_new[:]
+
+        def columns(half):
+            return slice(BANK * half, BANK * (half + 1))
+
+        def product(a, half):
+            x_mu = turn_back(MU_BLOCK, half, a)
+            nc.vector.tensor_tensor(
+                out=mu_new_of[a][:, :, columns(half)],
+                in0=x_mu[:].unsqueeze(1).to_broadcast([P, XYZ, BANK]),
+                in1=muW_of[a][:, :, columns(half)],
+                op=MULT,
+            )
+
+        def gpsimd_sum(a, half):
+            cols = columns(half)
+            nc.gpsimd.tensor_tensor(out=mu_new_of[a][:, :, cols], in0=mu_new_of[a][:, :, cols], in1=mu_of[a][:, :, cols], op=ADD)
+
+        steps = (
+            (((0, 0), (1, 0)), 1),
+            (((0, 1), (1, 1)), 1),
+            (((2, 0), (3, 0)), 2),
+            (((2, 1), (3, 1)), 1),
+        )
+        made = 1
+        for half_tiles, blocks_behind in steps:
+            for a, half in half_tiles:
+                product(a, half)
+            for a, half in half_tiles:
+                if (a, half) in VECTOR_HALF_TILES:
+                    continue
+                gpsimd_sum(a, half)
+                if a == 1:
+                    nc.sync.dma_start(
+                        out=mu_out_rows[:, 0:2, :, columns(half)].rearrange("p a c f -> p (a c) f"),
+                        in_=mu_new_01[:, :, :, columns(half)].rearrange("p a c f -> p (a c) f"),
                     )
-                for a in (2 * pair, 2 * pair + 1):
-                    if (a, half) not in VECTOR_HALF_TILES:
-                        nc.gpsimd.tensor_tensor(out=mu_new_of[a][:, :, cols], in0=mu_new_of[a][:, :, cols], in1=mu_tiles[a][:, :, cols], op=ADD)
-                        nc.sync.dma_start(out=mu_out_rows[:, a, :, cols], in_=mu_new_of[a][:, :, cols])
-                for n in range(made_behind[pair, half]):
-                    make_x_columns(*x_order[made])
-                    made += 1
+                if a > 1:
+                    nc.sync.dma_start(out=mu_out_rows[:, a, :, columns(half)], in_=mu_new_of[a][:, :, columns(half)])
+            for n in range(blocks_behind):
+                make_x_columns(*x_order[made])
+                made += 1
 
         def vector_sum(a, half, c):
-            cols = slice(BANK * half, BANK * (half + 1))
+            cols = columns(half)
             mu_f32 = psum.tile([P, BANK], F32, tag="bank")
-            nc.tensor.matmul(out=mu_f32[:], lhsT=ident_bf[:], rhs=mu_tiles[a][:, c, cols], start=True, stop=True)
+            nc.tensor.matmul(out=mu_f32[:], lhsT=ident_bf[:], rhs=mu_of[a][:, c, cols], start=True, stop=True)
             nc.vector.tensor_tensor(out=mu_new_of[a][:, c, cols], in0=mu_f32[:], in1=mu_new_of[a][:, c, cols], op=ADD)
             if c == XYZ - 1:
                 nc.scalar.dma_start(out=mu_out_rows[:, a, :, cols], in_=mu_new_of[a][:, :, cols])
 
         vector_sums = [(a, half, c) for (a, half) in VECTOR_HALF_TILES for c in range(XYZ)]
         q_out_rows = out_0.rearrange("(p a) o f -> p a (o f)", a=ATOM_TILES)
+        q_new = keep.tile([P, ATOM_TILES, F], F32)
         for a in range(ATOM_TILES):
             for job in vector_sums[SUMS_A_STEP * a : SUMS_A_STEP * (a + 1)]:
                 vector_sum(*job)
-            q_new = q_results.tile([P, F], F32)
             for half in range(HALVES):
-                cols = slice(BANK * half, BANK * (half + 1))
                 x_gate = turn_back(GATE_BLOCK, half, a)
-                nc.vector.tensor_tensor(out=q_new[:, cols], in0=x_gate[:], in1=gate_sb[:, a, cols], op=MULT)
+                nc.vector.tensor_tensor(out=q_new[:, a, columns(half)], in0=x_gate[:], in1=gate_sb[:, a, columns(half)], op=MULT)
             for half in range(HALVES):
-                cols = slice(BANK * half, BANK * (half + 1))
+                cols = columns(half)
                 q_plus_x = turn_back(Q_BLOCK, half, a, onto=q_sb[:, a, cols])
-                nc.vector.tensor_tensor(out=q_new[:, cols], in0=q_plus_x[:], in1=q_new[:, cols], op=ADD)
-                nc.scalar.dma_start(out=q_out_rows[:, a, cols], in_=q_new[:, cols])
+                nc.vector.tensor_tensor(out=q_new[:, a, cols], in0=q_plus_x[:], in1=q_new[:, a, cols], op=ADD)
+                if a == ATOM_TILES - 1:
+                    nc.scalar.dma_start(out=q_out_rows[:, a, cols], in_=q_new[:, a, cols])
+            if a < ATOM_TILES - 1:
+                nc.scalar.dma_start(out=q_out_rows[:, a, :], in_=q_new[:, a, :])

@@ -32,7 +32,7 @@ HALVES = F // BANK
 CHANNEL_TILES = 3 * F // P
 TILES_PER_BANK = BANK // P
 VECTOR_HALF_TILES = ((2, 1), (3, 1))
-SUMS_A_STEP = 2
+SUMS_A_STEP = 3
 SINGLE_TILES = 2
 
 FLOPS = 2 * ATOMS * K * 3 * F
@@ -43,7 +43,7 @@ def tile_painnmixing_pb_kernel(tc, h, mu_W, mu_VW, q, mu, W2_words, W2_scales, b
     with ExitStack() as ctx:
         keep = ctx.enter_context(tc.tile_pool(name="keep", bufs=1))
         inputs = ctx.enter_context(tc.tile_pool(name="inputs", bufs=SINGLE_TILES))
-        mu_results = ctx.enter_context(tc.tile_pool(name="mu_results", bufs=2))
+        mu_results = ctx.enter_context(tc.tile_pool(name="mu_results", bufs=ATOM_TILES))
         psum = ctx.enter_context(tc.psum_pool(name="psum", bufs=PSUM_BANKS))
         ctx.enter_context(tc.manual_schedule())
 
@@ -178,9 +178,8 @@ def tile_painnmixing_pb_kernel(tc, h, mu_W, mu_VW, q, mu, W2_words, W2_scales, b
         make_x_columns(*x_order[0], vector_helps=True)
 
         mu_out_rows = out_1.rearrange("(p a) c f -> p a c f", a=ATOM_TILES)
-        mu_new_01 = keep.tile([P, 2, XYZ, F], F32)
-        mu_new_of = {0: mu_new_01[:, 0], 1: mu_new_01[:, 1]}
-        for a in (2, 3):
+        mu_new_of = {}
+        for a in range(ATOM_TILES):
             mu_new = mu_results.tile([P, XYZ, F], F32)
             mu_new_of[a] = mu_new[:]
 
@@ -200,27 +199,23 @@ def tile_painnmixing_pb_kernel(tc, h, mu_W, mu_VW, q, mu, W2_words, W2_scales, b
             cols = columns(half)
             nc.gpsimd.tensor_tensor(out=mu_new_of[a][:, :, cols], in0=mu_new_of[a][:, :, cols], in1=mu_of[a][:, :, cols], op=ADD)
 
+        def store_mu(a):
+            nc.sync.dma_start(out=mu_out_rows[:, a], in_=mu_new_of[a])
+
         steps = (
-            (((0, 0), (1, 0)), 1),
-            (((0, 1), (1, 1)), 1),
-            (((2, 0), (3, 0)), 2),
-            (((2, 1), (3, 1)), 1),
+            (((0, 0), (1, 0)), ((0, 0), (1, 0)), 1),
+            (((0, 1), (1, 1)), ((0, 1), (1, 1)), 1),
+            (((2, 0), (3, 0)), ((2, 0), (3, 0)), 2),
+            (((2, 1), (3, 1)), (), 1),
         )
         made = 1
-        for half_tiles, blocks_behind in steps:
-            for a, half in half_tiles:
+        for products, sums, blocks_behind in steps:
+            for a, half in products:
                 product(a, half)
-            for a, half in half_tiles:
-                if (a, half) in VECTOR_HALF_TILES:
-                    continue
+            for a, half in sums:
                 gpsimd_sum(a, half)
-                if a == 1:
-                    nc.sync.dma_start(
-                        out=mu_out_rows[:, 0:2, :, columns(half)].rearrange("p a c f -> p (a c) f"),
-                        in_=mu_new_01[:, :, :, columns(half)].rearrange("p a c f -> p (a c) f"),
-                    )
-                if a > 1:
-                    nc.sync.dma_start(out=mu_out_rows[:, a, :, columns(half)], in_=mu_new_of[a][:, :, columns(half)])
+                if half == HALVES - 1:
+                    store_mu(a)
             for n in range(blocks_behind):
                 make_x_columns(*x_order[made])
                 made += 1
@@ -231,7 +226,7 @@ def tile_painnmixing_pb_kernel(tc, h, mu_W, mu_VW, q, mu, W2_words, W2_scales, b
             nc.tensor.matmul(out=mu_f32[:], lhsT=ident_bf[:], rhs=mu_of[a][:, c, cols], start=True, stop=True)
             nc.vector.tensor_tensor(out=mu_new_of[a][:, c, cols], in0=mu_f32[:], in1=mu_new_of[a][:, c, cols], op=ADD)
             if c == XYZ - 1:
-                nc.scalar.dma_start(out=mu_out_rows[:, a, :, cols], in_=mu_new_of[a][:, :, cols])
+                store_mu(a)
 
         vector_sums = [(a, half, c) for (a, half) in VECTOR_HALF_TILES for c in range(XYZ)]
         q_out_rows = out_0.rearrange("(p a) o f -> p a (o f)", a=ATOM_TILES)

@@ -57,10 +57,14 @@ def tile_painnmixing_pb_kernel(tc, h, mu_W, mu_VW, q, mu, W2_words, W2_scales, b
         for pair in range(ATOM_TILES // 2):
             nc.sync.dma_start(out=h_sb[:, 2 * pair : 2 * pair + 2, :], in_=h_rows[:, 2 * pair : 2 * pair + 2, :])
 
-        w_planes = keep.tile([P, PASSES, 3 * F], U8, align_bytes=64)
-        nc.vector.memset(w_planes[:].bitcast(I32), 0)
+        w_planes = {}
         bias_bf = keep.tile([P, P], BF16)
-        nc.vector.memset(bias_bf[:], 0.0)
+        for block in (MU_BLOCK, GATE_BLOCK, Q_BLOCK):
+            planes = keep.tile([P, PASSES, F], U8, align_bytes=64, tag="planes%d" % block)
+            nc.vector.memset(planes[:].bitcast(I32), 0)
+            w_planes[block] = planes
+            if block == MU_BLOCK:
+                nc.vector.memset(bias_bf[:], 0.0)
         nc.scalar.dma_start(out=bias_bf[:CHANNEL_TILES, :], in_=b2.rearrange("(j c) -> j c", c=P))
 
         word_rows = W2_words.rearrange("g p b -> p g b")
@@ -71,10 +75,13 @@ def tile_painnmixing_pb_kernel(tc, h, mu_W, mu_VW, q, mu, W2_words, W2_scales, b
             words = keep.tile([P, PASSES, 2 * F], U8, align_bytes=64, tag="words%d" % block)
             nc.sync.dma_start(out=words[:].bitcast(I32), in_=word_rows[:, :, 2 * F * block : 2 * F * (block + 1)].bitcast(I32))
             w_words[block] = words
+            for i in range(4):
+                nc.sync.dma_start(
+                    out=w_planes[block][i:P:32].bitcast(I32),
+                    in_=scale_rows[i:16:4, :, F * block : F * (block + 1)].bitcast(I32),
+                )
 
         load_words(MU_BLOCK)
-        for i in range(4):
-            nc.sync.dma_start(out=w_planes[i:P:32].bitcast(I32), in_=scale_rows[i:16:4].bitcast(I32))
 
         muW_rows = mu_W.rearrange("(p a) c f -> p a c f", a=ATOM_TILES)
         mu_rows = mu.rearrange("(p a) c f -> p a c f", a=ATOM_TILES)
@@ -140,17 +147,20 @@ def tile_painnmixing_pb_kernel(tc, h, mu_W, mu_VW, q, mu, W2_words, W2_scales, b
             for i in range(TILES_PER_BANK):
                 acc = psum.tile([P, ATOMS], F32, tag="bank")
                 accs.append(acc)
-            for g in range(PASSES):
-                for i in range(TILES_PER_BANK):
-                    nc.tensor.matmul_mx(
-                        out=accs[i][:],
-                        lhsT=w_words[block][:, g, 2 * P * (first_tile + i) : 2 * P * (first_tile + i + 1)].bitcast(FP4X4),
-                        lhsT_scale=w_planes[:, g, F * block + P * (first_tile + i) : F * block + P * (first_tile + i + 1)],
-                        rhs=h_codes[:, g, :].bitcast(FP8X4),
-                        rhs_scale=h_scales[:, g, :],
-                        start=(g == 0),
-                        stop=(g == PASSES - 1),
-                    )
+            if vector_helps:
+                order = [(g, i) for g in range(PASSES) for i in range(TILES_PER_BANK)]
+            else:
+                order = [(g, i) for i in range(TILES_PER_BANK) for g in range(PASSES)]
+            for g, i in order:
+                nc.tensor.matmul_mx(
+                    out=accs[i][:],
+                    lhsT=w_words[block][:, g, 2 * P * (first_tile + i) : 2 * P * (first_tile + i + 1)].bitcast(FP4X4),
+                    lhsT_scale=w_planes[block][:, g, P * (first_tile + i) : P * (first_tile + i + 1)],
+                    rhs=h_codes[:, g, :].bitcast(FP8X4),
+                    rhs_scale=h_scales[:, g, :],
+                    start=(g == 0),
+                    stop=(g == PASSES - 1),
+                )
             for i in range(TILES_PER_BANK):
                 j = F // P * block + first_tile + i
                 if vector_helps and i % 2 == 1:

@@ -33,6 +33,7 @@ CHANNEL_TILES = 3 * F // P
 TILES_PER_BANK = BANK // P
 VECTOR_HALF_TILES = ((2, 1), (3, 1))
 SUMS_A_STEP = 3
+DMA_ALIGN = 256
 SINGLE_TILES = 2
 
 FLOPS = 2 * ATOMS * K * 3 * F
@@ -52,15 +53,15 @@ def tile_painnmixing_pb_kernel(tc, h, mu_W, mu_VW, q, mu, W2_words, W2_scales, b
         ident_bf = keep.tile([P, P], BF16)
         make_identity(nc, ident_bf[:])
 
-        h_sb = keep.tile([P, ATOM_TILES, K], BF16)
+        h_sb = keep.tile([P, ATOM_TILES, K], BF16, align_bytes=DMA_ALIGN)
         h_rows = h.rearrange("(p a) o k -> p a (o k)", a=ATOM_TILES)
         for pair in range(ATOM_TILES // 2):
             nc.sync.dma_start(out=h_sb[:, 2 * pair : 2 * pair + 2, :], in_=h_rows[:, 2 * pair : 2 * pair + 2, :])
 
         w_planes = {}
-        bias_bf = keep.tile([P, P], BF16)
+        bias_bf = keep.tile([P, P], BF16, align_bytes=DMA_ALIGN)
         for block in (MU_BLOCK, GATE_BLOCK, Q_BLOCK):
-            planes = keep.tile([P, PASSES, F], U8, align_bytes=64, tag="planes%d" % block)
+            planes = keep.tile([P, PASSES, F], U8, align_bytes=DMA_ALIGN, tag="planes%d" % block)
             nc.vector.memset(planes[:].bitcast(I32), 0)
             w_planes[block] = planes
             if block == MU_BLOCK:
@@ -72,7 +73,7 @@ def tile_painnmixing_pb_kernel(tc, h, mu_W, mu_VW, q, mu, W2_words, W2_scales, b
         w_words = {}
 
         def load_words(block):
-            words = keep.tile([P, PASSES, 2 * F], U8, align_bytes=64, tag="words%d" % block)
+            words = keep.tile([P, PASSES, 2 * F], U8, align_bytes=DMA_ALIGN, tag="words%d" % block)
             nc.sync.dma_start(out=words[:].bitcast(I32), in_=word_rows[:, :, 2 * F * block : 2 * F * (block + 1)].bitcast(I32))
             w_words[block] = words
             for i in range(4):
@@ -87,23 +88,23 @@ def tile_painnmixing_pb_kernel(tc, h, mu_W, mu_VW, q, mu, W2_words, W2_scales, b
         mu_rows = mu.rearrange("(p a) c f -> p a c f", a=ATOM_TILES)
         muW_of, mu_of = {}, {}
         for a in range(SINGLE_TILES):
-            muW_a = inputs.tile([P, XYZ, F], BF16)
+            muW_a = inputs.tile([P, XYZ, F], BF16, align_bytes=DMA_ALIGN)
             nc.sync.dma_start(out=muW_a[:], in_=muW_rows[:, a])
             muW_of[a] = muW_a[:]
-            mu_a = inputs.tile([P, XYZ, F], BF16)
+            mu_a = inputs.tile([P, XYZ, F], BF16, align_bytes=DMA_ALIGN)
             nc.sync.dma_start(out=mu_a[:], in_=mu_rows[:, a])
             mu_of[a] = mu_a[:]
         load_words(GATE_BLOCK)
-        muW_rest = keep.tile([P, ATOM_TILES - SINGLE_TILES, XYZ, F], BF16)
+        muW_rest = keep.tile([P, ATOM_TILES - SINGLE_TILES, XYZ, F], BF16, align_bytes=DMA_ALIGN)
         nc.sync.dma_start(out=muW_rest[:], in_=muW_rows[:, SINGLE_TILES:])
         load_words(Q_BLOCK)
-        mu_rest = keep.tile([P, ATOM_TILES - SINGLE_TILES, XYZ, F], BF16)
+        mu_rest = keep.tile([P, ATOM_TILES - SINGLE_TILES, XYZ, F], BF16, align_bytes=DMA_ALIGN)
         nc.sync.dma_start(out=mu_rest[:], in_=mu_rows[:, SINGLE_TILES:])
         for a in range(SINGLE_TILES, ATOM_TILES):
             muW_of[a] = muW_rest[:, a - SINGLE_TILES]
             mu_of[a] = mu_rest[:, a - SINGLE_TILES]
-        gate_sb = keep.tile([P, ATOM_TILES, F], BF16)
-        q_sb = keep.tile([P, ATOM_TILES, F], BF16)
+        gate_sb = keep.tile([P, ATOM_TILES, F], BF16, align_bytes=DMA_ALIGN)
+        q_sb = keep.tile([P, ATOM_TILES, F], BF16, align_bytes=DMA_ALIGN)
         nc.sync.dma_start(out=gate_sb[:], in_=mu_VW.rearrange("(p a) o f -> p a (o f)", a=ATOM_TILES))
         nc.sync.dma_start(out=q_sb[:], in_=q.rearrange("(p a) o f -> p a (o f)", a=ATOM_TILES))
 
@@ -190,7 +191,7 @@ def tile_painnmixing_pb_kernel(tc, h, mu_W, mu_VW, q, mu, W2_words, W2_scales, b
         mu_out_rows = out_1.rearrange("(p a) c f -> p a c f", a=ATOM_TILES)
         mu_new_of = {}
         for a in range(ATOM_TILES):
-            mu_new = mu_results.tile([P, XYZ, F], F32)
+            mu_new = mu_results.tile([P, XYZ, F], F32, align_bytes=DMA_ALIGN)
             mu_new_of[a] = mu_new[:]
 
         def columns(half):
@@ -240,7 +241,7 @@ def tile_painnmixing_pb_kernel(tc, h, mu_W, mu_VW, q, mu, W2_words, W2_scales, b
 
         vector_sums = [(a, half, c) for (a, half) in VECTOR_HALF_TILES for c in range(XYZ)]
         q_out_rows = out_0.rearrange("(p a) o f -> p a (o f)", a=ATOM_TILES)
-        q_new = keep.tile([P, ATOM_TILES, F], F32)
+        q_new = keep.tile([P, ATOM_TILES, F], F32, align_bytes=DMA_ALIGN)
         for a in range(ATOM_TILES):
             for job in vector_sums[SUMS_A_STEP * a : SUMS_A_STEP * (a + 1)]:
                 vector_sum(*job)

@@ -34,7 +34,6 @@ TILES_PER_BANK = BANK // P
 VECTOR_HALF_TILES = ((2, 1), (3, 1))
 SUMS_A_STEP = 3
 DMA_ALIGN = 256
-SINGLE_TILES = 2
 
 FLOPS = 2 * ATOMS * K * 3 * F
 
@@ -43,7 +42,6 @@ def tile_painnmixing_pb_kernel(tc, h, mu_W, mu_VW, q, mu, W2_words, W2_scales, b
     nc = tc.nc
     with ExitStack() as ctx:
         keep = ctx.enter_context(tc.tile_pool(name="keep", bufs=1))
-        inputs = ctx.enter_context(tc.tile_pool(name="inputs", bufs=SINGLE_TILES))
         mu_results = ctx.enter_context(tc.tile_pool(name="mu_results", bufs=ATOM_TILES))
         psum = ctx.enter_context(tc.psum_pool(name="psum", bufs=PSUM_BANKS))
         ctx.enter_context(tc.manual_schedule())
@@ -87,22 +85,19 @@ def tile_painnmixing_pb_kernel(tc, h, mu_W, mu_VW, q, mu, W2_words, W2_scales, b
         muW_rows = mu_W.rearrange("(p a) c f -> p a c f", a=ATOM_TILES)
         mu_rows = mu.rearrange("(p a) c f -> p a c f", a=ATOM_TILES)
         muW_of, mu_of = {}, {}
-        for a in range(SINGLE_TILES):
-            muW_a = inputs.tile([P, XYZ, F], BF16, align_bytes=DMA_ALIGN)
-            nc.sync.dma_start(out=muW_a[:], in_=muW_rows[:, a])
-            muW_of[a] = muW_a[:]
-            mu_a = inputs.tile([P, XYZ, F], BF16, align_bytes=DMA_ALIGN)
-            nc.sync.dma_start(out=mu_a[:], in_=mu_rows[:, a])
-            mu_of[a] = mu_a[:]
+
+        def load_pair(rows, views, pair, name):
+            both = keep.tile([P, 2, XYZ, F], BF16, align_bytes=DMA_ALIGN, tag="%s%d" % (name, pair))
+            nc.sync.dma_start(out=both[:], in_=rows[:, 2 * pair : 2 * pair + 2])
+            for j in range(2):
+                views[2 * pair + j] = both[:, j]
+
+        load_pair(muW_rows, muW_of, 0, "muW")
+        load_pair(mu_rows, mu_of, 0, "mu")
         load_words(GATE_BLOCK)
-        muW_rest = keep.tile([P, ATOM_TILES - SINGLE_TILES, XYZ, F], BF16, align_bytes=DMA_ALIGN)
-        nc.sync.dma_start(out=muW_rest[:], in_=muW_rows[:, SINGLE_TILES:])
+        load_pair(muW_rows, muW_of, 1, "muW")
         load_words(Q_BLOCK)
-        mu_rest = keep.tile([P, ATOM_TILES - SINGLE_TILES, XYZ, F], BF16, align_bytes=DMA_ALIGN)
-        nc.sync.dma_start(out=mu_rest[:], in_=mu_rows[:, SINGLE_TILES:])
-        for a in range(SINGLE_TILES, ATOM_TILES):
-            muW_of[a] = muW_rest[:, a - SINGLE_TILES]
-            mu_of[a] = mu_rest[:, a - SINGLE_TILES]
+        load_pair(mu_rows, mu_of, 1, "mu")
         gate_sb = keep.tile([P, ATOM_TILES, F], BF16, align_bytes=DMA_ALIGN)
         q_sb = keep.tile([P, ATOM_TILES, F], BF16, align_bytes=DMA_ALIGN)
         nc.sync.dma_start(out=gate_sb[:], in_=mu_VW.rearrange("(p a) o f -> p a (o f)", a=ATOM_TILES))
@@ -252,7 +247,7 @@ def tile_painnmixing_pb_kernel(tc, h, mu_W, mu_VW, q, mu, W2_words, W2_scales, b
                 cols = columns(half)
                 q_plus_x = turn_back(Q_BLOCK, half, a, onto=q_sb[:, a, cols])
                 nc.vector.tensor_tensor(out=q_new[:, a, cols], in0=q_plus_x[:], in1=q_new[:, a, cols], op=ADD)
-                if a == ATOM_TILES - 1:
-                    nc.scalar.dma_start(out=q_out_rows[:, a, cols], in_=q_new[:, a, cols])
-            if a < ATOM_TILES - 1:
+            if a == 1:
+                nc.scalar.dma_start(out=q_out_rows[:, 0:2, :], in_=q_new[:, 0:2, :])
+            if a > 1:
                 nc.scalar.dma_start(out=q_out_rows[:, a, :], in_=q_new[:, a, :])

@@ -31,8 +31,6 @@ PSUM_BANKS = 8
 HALVES = F // BANK
 CHANNEL_TILES = 3 * F // P
 TILES_PER_BANK = BANK // P
-VECTOR_HALF_TILES = ((2, 1), (3, 1))
-SUMS_A_STEP = 3
 DMA_ALIGN = 256
 
 FLOPS = 2 * ATOMS * K * 3 * F
@@ -42,7 +40,7 @@ def tile_painnmixing_pb_kernel(tc, h, mu_W, mu_VW, q, mu, W2_words, W2_scales, b
     nc = tc.nc
     with ExitStack() as ctx:
         keep = ctx.enter_context(tc.tile_pool(name="keep", bufs=1))
-        mu_results = ctx.enter_context(tc.tile_pool(name="mu_results", bufs=ATOM_TILES))
+        mu_results = ctx.enter_context(tc.tile_pool(name="mu_results", bufs=ATOM_TILES // 2))
         psum = ctx.enter_context(tc.psum_pool(name="psum", bufs=PSUM_BANKS))
         ctx.enter_context(tc.manual_schedule())
 
@@ -184,10 +182,12 @@ def tile_painnmixing_pb_kernel(tc, h, mu_W, mu_VW, q, mu, W2_words, W2_scales, b
         make_x_columns(*x_order[0], vector_helps=True)
 
         mu_out_rows = out_1.rearrange("(p a) c f -> p a c f", a=ATOM_TILES)
-        mu_new_of = {}
-        for a in range(ATOM_TILES):
-            mu_new = mu_results.tile([P, XYZ, F], F32, align_bytes=DMA_ALIGN)
-            mu_new_of[a] = mu_new[:]
+        mu_new_of, mu_new_pairs = {}, []
+        for pair in range(ATOM_TILES // 2):
+            mu_new = mu_results.tile([P, 2, XYZ, F], F32, align_bytes=DMA_ALIGN)
+            mu_new_pairs.append(mu_new)
+            for j in range(2):
+                mu_new_of[2 * pair + j] = mu_new[:, j]
 
         def columns(half):
             return slice(BANK * half, BANK * (half + 1))
@@ -205,41 +205,37 @@ def tile_painnmixing_pb_kernel(tc, h, mu_W, mu_VW, q, mu, W2_words, W2_scales, b
             cols = columns(half)
             nc.gpsimd.tensor_tensor(out=mu_new_of[a][:, :, cols], in0=mu_new_of[a][:, :, cols], in1=mu_of[a][:, :, cols], op=ADD)
 
-        def store_mu(a):
-            nc.sync.dma_start(out=mu_out_rows[:, a], in_=mu_new_of[a])
+        def vector_sum(a, half):
+            cols = columns(half)
+            for c in range(XYZ):
+                mu_f32 = psum.tile([P, BANK], F32, tag="bank")
+                nc.tensor.matmul(out=mu_f32[:], lhsT=ident_bf[:], rhs=mu_of[a][:, c, cols], start=True, stop=True)
+                nc.vector.tensor_tensor(out=mu_new_of[a][:, c, cols], in0=mu_f32[:], in1=mu_new_of[a][:, c, cols], op=ADD)
 
         steps = (
-            (((0, 0), (1, 0)), ((0, 0), (1, 0)), 1),
-            (((0, 1), (1, 1)), ((0, 1), (1, 1)), 1),
-            (((2, 0), (3, 0)), ((2, 0), (3, 0)), 2),
-            (((2, 1), (3, 1)), (), 1),
+            (((0, 0), (1, 0)), ((0, 0), (1, 0)), (), 1),
+            (((0, 1), (1, 1)), ((0, 1),), (), 1),
+            (((2, 0), (3, 0)), ((2, 0),), ((1, 1),), 2),
+            (((2, 1), (3, 1)), ((2, 1), (3, 0)), ((3, 1),), 1),
         )
         made = 1
-        for products, sums, blocks_behind in steps:
+        for products, gpsimd_sums, vector_sums, blocks_behind in steps:
             for a, half in products:
                 product(a, half)
-            for a, half in sums:
+            for a, half in gpsimd_sums:
                 gpsimd_sum(a, half)
-                if half == HALVES - 1:
-                    store_mu(a)
+            for a, half in vector_sums:
+                vector_sum(a, half)
             for n in range(blocks_behind):
                 make_x_columns(*x_order[made])
                 made += 1
+        nc.sync.dma_start(out=mu_out_rows[:, 0:2], in_=mu_new_pairs[0][:])
+        for j in range(2):
+            nc.sync.dma_start(out=mu_out_rows[:, 2 + j], in_=mu_new_pairs[1][:, j])
 
-        def vector_sum(a, half, c):
-            cols = columns(half)
-            mu_f32 = psum.tile([P, BANK], F32, tag="bank")
-            nc.tensor.matmul(out=mu_f32[:], lhsT=ident_bf[:], rhs=mu_of[a][:, c, cols], start=True, stop=True)
-            nc.vector.tensor_tensor(out=mu_new_of[a][:, c, cols], in0=mu_f32[:], in1=mu_new_of[a][:, c, cols], op=ADD)
-            if c == XYZ - 1:
-                store_mu(a)
-
-        vector_sums = [(a, half, c) for (a, half) in VECTOR_HALF_TILES for c in range(XYZ)]
         q_out_rows = out_0.rearrange("(p a) o f -> p a (o f)", a=ATOM_TILES)
         q_new = keep.tile([P, ATOM_TILES, F], F32, align_bytes=DMA_ALIGN)
         for a in range(ATOM_TILES):
-            for job in vector_sums[SUMS_A_STEP * a : SUMS_A_STEP * (a + 1)]:
-                vector_sum(*job)
             for half in range(HALVES):
                 x_gate = turn_back(GATE_BLOCK, half, a)
                 nc.vector.tensor_tensor(out=q_new[:, a, columns(half)], in0=x_gate[:], in1=gate_sb[:, a, columns(half)], op=MULT)
@@ -247,7 +243,5 @@ def tile_painnmixing_pb_kernel(tc, h, mu_W, mu_VW, q, mu, W2_words, W2_scales, b
                 cols = columns(half)
                 q_plus_x = turn_back(Q_BLOCK, half, a, onto=q_sb[:, a, cols])
                 nc.vector.tensor_tensor(out=q_new[:, a, cols], in0=q_plus_x[:], in1=q_new[:, a, cols], op=ADD)
-            if a == 1:
-                nc.scalar.dma_start(out=q_out_rows[:, 0:2, :], in_=q_new[:, 0:2, :])
-            if a > 1:
-                nc.scalar.dma_start(out=q_out_rows[:, a, :], in_=q_new[:, a, :])
+            if a % 2 == 1:
+                nc.scalar.dma_start(out=q_out_rows[:, a - 1 : a + 1, :], in_=q_new[:, a - 1 : a + 1, :])

from contextlib import ExitStack

import concourse.mybir as mybir
from concourse.masks import make_identity

F32 = mybir.dt.float32
BF16 = mybir.dt.bfloat16
I32 = mybir.dt.int32
U32 = mybir.dt.uint32
U8 = mybir.dt.uint8
FP8X4 = mybir.dt.float8_e4m3fn_x4
FP4X4 = mybir.dt.float4_e2m1fn_x4
ADD = mybir.AluOpType.add
MULT = mybir.AluOpType.mult
IDENTITY = mybir.ActivationFunctionType.Identity

P = 128
ATOMS = 512
ATOM_TILES = ATOMS // P
K = 1024
K_PASS = 4 * P
PASSES = K // K_PASS
WORDS_PER_PASS = K_PASS // 2
F = 1024
Q_BLOCK = 0
MU_BLOCK = 1
GATE_BLOCK = 2
XYZ = 3
BANK = 512
PSUM_BANKS = 8
HALVES = F // BANK
CHANNEL_TILES = 3 * F // P
TILES_PER_BANK = BANK // P
DMA_ALIGN = 256

FLOPS = 2 * ATOMS * K * 3 * F


def tile_painnmixing_pb_kernel(tc, h, mu_W, mu_VW, q, mu, W2_words, W2_scales, b2, out_0, out_1):
    nc = tc.nc
    with ExitStack() as ctx:
        keep = ctx.enter_context(tc.tile_pool(name="keep", bufs=1))
        mu_results = ctx.enter_context(tc.tile_pool(name="mu_results", bufs=ATOM_TILES // 2))
        psum = ctx.enter_context(tc.psum_pool(name="psum", bufs=PSUM_BANKS))
        ctx.enter_context(tc.manual_schedule())

        ident = keep.tile([P, P], F32)
        make_identity(nc, ident[:])
        ident_bf = keep.tile([P, P], BF16)
        make_identity(nc, ident_bf[:])

        h_sb = keep.tile([P, ATOM_TILES, K], BF16, align_bytes=DMA_ALIGN)
        h_rows = h.rearrange("(p a) o k -> p a (o k)", a=ATOM_TILES)
        for pair in range(ATOM_TILES // 2):
            nc.sync.dma_start(out=h_sb[:, 2 * pair : 2 * pair + 2, :], in_=h_rows[:, 2 * pair : 2 * pair + 2, :])

        w_planes = {}
        bias_bf = keep.tile([P, P], BF16, align_bytes=DMA_ALIGN)
        for block in (MU_BLOCK, GATE_BLOCK, Q_BLOCK):
            planes = keep.tile([P, PASSES, F], U8, align_bytes=DMA_ALIGN, tag="planes%d" % block)
            nc.vector.memset(planes[:].bitcast(I32), 0)
            w_planes[block] = planes
            if block == MU_BLOCK:
                nc.vector.memset(bias_bf[:], 0.0)
        nc.scalar.dma_start(out=bias_bf[:CHANNEL_TILES, :], in_=b2.rearrange("(j c) -> j c", c=P))

        word_rows = W2_words.rearrange("g p b -> p g b")
        scale_rows = W2_scales.rearrange("g r n -> r g n")
        w_words = {}

        def load_words(block):
            words = keep.tile([P, PASSES, 2 * F], U8, align_bytes=DMA_ALIGN, tag="words%d" % block)
            nc.sync.dma_start(out=words[:].bitcast(I32), in_=word_rows[:, :, 2 * F * block : 2 * F * (block + 1)].bitcast(I32))
            w_words[block] = words
            for i in range(4):
                nc.sync.dma_start(
                    out=w_planes[block][i:P:32].bitcast(I32),
                    in_=scale_rows[i:16:4, :, F * block : F * (block + 1)].bitcast(I32),
                )

        load_words(MU_BLOCK)

        muW_rows = mu_W.rearrange("(p a) c f -> p a c f", a=ATOM_TILES)
        mu_rows = mu.rearrange("(p a) c f -> p a c f", a=ATOM_TILES)
        muW_of, mu_of = {}, {}

        def load_pair(rows, views, pair, name):
            both = keep.tile([P, 2, XYZ, F], BF16, align_bytes=DMA_ALIGN, tag="%s%d" % (name, pair))
            nc.sync.dma_start(out=both[:], in_=rows[:, 2 * pair : 2 * pair + 2])
            for j in range(2):
                views[2 * pair + j] = both[:, j]

        load_pair(muW_rows, muW_of, 0, "muW")
        load_pair(mu_rows, mu_of, 0, "mu")
        load_words(GATE_BLOCK)
        load_pair(muW_rows, muW_of, 1, "muW")
        load_words(Q_BLOCK)
        load_pair(mu_rows, mu_of, 1, "mu")
        gate_sb = keep.tile([P, ATOM_TILES, F], BF16, align_bytes=DMA_ALIGN)
        q_sb = keep.tile([P, ATOM_TILES, F], BF16, align_bytes=DMA_ALIGN)
        nc.sync.dma_start(out=gate_sb[:], in_=mu_VW.rearrange("(p a) o f -> p a (o f)", a=ATOM_TILES))
        nc.sync.dma_start(out=q_sb[:], in_=q.rearrange("(p a) o f -> p a (o f)", a=ATOM_TILES))

        h_codes = keep.tile([P, PASSES, ATOMS], U32, align_bytes=64)
        h_scales = keep.tile([P, PASSES, ATOMS], U8, align_bytes=64)
        h_words = h_sb[:].bitcast(F32)
        for pair in range(ATOM_TILES // 2):
            atoms = slice(2 * P * pair, 2 * P * (pair + 1))
            for g in range(PASSES):
                turned = psum.tile([P, 2, 2 * P], F32, tag="bank")
                for u in range(2):
                    for j in range(2):
                        nc.tensor.transpose(
                            turned[:, u, P * j : P * (j + 1)],
                            h_words[:, 2 * pair + j, WORDS_PER_PASS * g + u : WORDS_PER_PASS * (g + 1) : 2],
                            ident[:],
                        )
                grouped = keep.tile([P, 2 * P, 4], BF16, align_bytes=64, tag="grouped%d%d" % (pair, g))
                grouped_words = grouped[:].rearrange("p n t -> p (n t)").bitcast(F32).rearrange("p (n u) -> p n u", u=2)
                if g == 0:
                    nc.scalar.copy(out=grouped_words, in_=turned[:].rearrange("p u n -> p n u"))
                else:
                    nc.vector.tensor_copy(out=grouped_words, in_=turned[:].rearrange("p u n -> p n u"))
                nc.vector.quantize_mx(
                    out=h_codes[:, g, atoms].bitcast(FP8X4),
                    scales=h_scales[:, g, atoms],
                    in_=grouped[:].rearrange("p n t -> p (n t)"),
                )

        bias_turned = psum.tile([P, P], BF16, tag="bank")
        nc.tensor.transpose(bias_turned[:], bias_bf[:], ident_bf[:])
        bias_col = keep.tile([P, CHANNEL_TILES], F32)
        nc.scalar.activation(out=bias_col[:], in_=bias_turned[:, :CHANNEL_TILES], func=IDENTITY)

        x_cols_of = {}

        def make_x_columns(block, half, vector_helps=False):
            x_cols = keep.tile([P, TILES_PER_BANK, ATOMS], F32, tag="x_cols%d%d" % (block, half))
            first_tile = TILES_PER_BANK * half
            accs = []
            for i in range(TILES_PER_BANK):
                acc = psum.tile([P, ATOMS], F32, tag="bank")
                accs.append(acc)
            if vector_helps:
                order = [(g, i) for g in range(PASSES) for i in range(TILES_PER_BANK)]
            else:
                order = [(g, i) for i in range(TILES_PER_BANK) for g in range(PASSES)]
            for g, i in order:
                nc.tensor.matmul_mx(
                    out=accs[i][:],
                    lhsT=w_words[block][:, g, 2 * P * (first_tile + i) : 2 * P * (first_tile + i + 1)].bitcast(FP4X4),
                    lhsT_scale=w_planes[block][:, g, P * (first_tile + i) : P * (first_tile + i + 1)],
                    rhs=h_codes[:, g, :].bitcast(FP8X4),
                    rhs_scale=h_scales[:, g, :],
                    start=(g == 0),
                    stop=(g == PASSES - 1),
                )
            for i in range(TILES_PER_BANK):
                j = F // P * block + first_tile + i
                if vector_helps and i % 2 == 1:
                    nc.vector.tensor_scalar(out=x_cols[:, i, :], in0=accs[i][:], scalar1=bias_col[:, j : j + 1], scalar2=None, op0=ADD)
                else:
                    nc.scalar.activation(out=x_cols[:, i, :], in_=accs[i][:], func=IDENTITY, bias=bias_col[:, j : j + 1])
            x_cols_of[block, half] = x_cols

        def turn_back(block, half, a, onto=None):
            x_rows = psum.tile([P, BANK], F32, tag="bank")
            if onto is not None:
                nc.tensor.matmul(out=x_rows[:], lhsT=ident_bf[:], rhs=onto, start=True, stop=False)
            for i in range(TILES_PER_BANK):
                nc.tensor.matmul(
                    out=x_rows[:, P * i : P * (i + 1)],
                    lhsT=x_cols_of[block, half][:, i, P * a : P * (a + 1)],
                    rhs=ident[:],
                    is_transpose=True,
                    start=(onto is None),
                    stop=(onto is None or i == TILES_PER_BANK - 1),
                )
            return x_rows

        x_order = [(block, half) for block in (MU_BLOCK, GATE_BLOCK, Q_BLOCK) for half in range(HALVES)]
        make_x_columns(*x_order[0], vector_helps=True)

        mu_out_rows = out_1.rearrange("(p a) c f -> p a c f", a=ATOM_TILES)
        mu_new_of, mu_new_pairs = {}, []
        for pair in range(ATOM_TILES // 2):
            mu_new = mu_results.tile([P, 2, XYZ, F], F32, align_bytes=DMA_ALIGN)
            mu_new_pairs.append(mu_new)
            for j in range(2):
                mu_new_of[2 * pair + j] = mu_new[:, j]

        def columns(half):
            return slice(BANK * half, BANK * (half + 1))

        def product(a, half):
            x_mu = turn_back(MU_BLOCK, half, a)
            nc.vector.tensor_tensor(
                out=mu_new_of[a][:, :, columns(half)],
                in0=x_mu[:].unsqueeze(1).to_broadcast([P, XYZ, BANK]),
                in1=muW_of[a][:, :, columns(half)],
                op=MULT,
            )

        def gpsimd_sum(a, half):
            cols = columns(half)
            nc.gpsimd.tensor_tensor(out=mu_new_of[a][:, :, cols], in0=mu_new_of[a][:, :, cols], in1=mu_of[a][:, :, cols], op=ADD)

        def vector_sum(a, half):
            cols = columns(half)
            for c in range(XYZ):
                mu_f32 = psum.tile([P, BANK], F32, tag="bank")
                nc.tensor.matmul(out=mu_f32[:], lhsT=ident_bf[:], rhs=mu_of[a][:, c, cols], start=True, stop=True)
                nc.vector.tensor_tensor(out=mu_new_of[a][:, c, cols], in0=mu_f32[:], in1=mu_new_of[a][:, c, cols], op=ADD)

        steps = (
            (((0, 0), (1, 0)), ((0, 0), (1, 0)), (), 1),
            (((0, 1), (1, 1)), ((0, 1),), (), 1),
            (((2, 0), (3, 0)), ((2, 0),), ((1, 1),), 2),
            (((2, 1), (3, 1)), ((2, 1), (3, 0)), ((3, 1),), 1),
        )
        made = 1
        for products, gpsimd_sums, vector_sums, blocks_behind in steps:
            for a, half in products:
                product(a, half)
            for a, half in gpsimd_sums:
                gpsimd_sum(a, half)
            for a, half in vector_sums:
                vector_sum(a, half)
            for n in range(blocks_behind):
                make_x_columns(*x_order[made])
                made += 1
        nc.sync.dma_start(out=mu_out_rows[:, 0:2], in_=mu_new_pairs[0][:])
        for j in range(2):
            nc.sync.dma_start(out=mu_out_rows[:, 2 + j], in_=mu_new_pairs[1][:, j])

        q_out_rows = out_0.rearrange("(p a) o f -> p a (o f)", a=ATOM_TILES)
        q_new = keep.tile([P, ATOM_TILES, F], F32, align_bytes=DMA_ALIGN)
        for a in range(ATOM_TILES):
            for half in range(HALVES):
                x_gate = turn_back(GATE_BLOCK, half, a)
                nc.vector.tensor_tensor(out=q_new[:, a, columns(half)], in0=x_gate[:], in1=gate_sb[:, a, columns(half)], op=MULT)
            for half in range(HALVES):
                cols = columns(half)
                q_plus_x = turn_back(Q_BLOCK, half, a, onto=q_sb[:, a, cols])
                nc.vector.tensor_tensor(out=q_new[:, a, cols], in0=q_plus_x[:], in1=q_new[:, a, cols], op=ADD)
            if a % 2 == 1:
                nc.scalar.dma_start(out=q_out_rows[:, a - 1 : a + 1, :], in_=q_new[:, a - 1 : a + 1, :])
